import numpy as np
import ml_dtypes


def mxq(x, axis, fmt="e4m3"):
    dtype, down = {"e4m3": (ml_dtypes.float8_e4m3fn, 7), "e5m2": (ml_dtypes.float8_e5m2, 14)}[fmt]
    v = np.moveaxis(np.asarray(x, np.float32).astype(ml_dtypes.bfloat16).astype(np.float64), axis, -1)
    blocks = v.reshape(v.shape[:-1] + (-1, 32))
    amax = np.abs(blocks).max(-1, keepdims=True)
    byte = np.maximum(np.where(amax > 0, np.frexp(amax)[1] - 1 + 127, 0) - down, 1)
    scale = np.exp2(byte - 127.0)
    codes = (blocks / scale).astype(np.float32).astype(dtype).astype(np.float64)
    return np.moveaxis((codes * scale).reshape(v.shape), -1, axis)


WIDE = False


def mx_kscale(k):
    if not WIDE:
        return np.ones(k)
    levels = np.array([10, -10, 5, -5, 0])
    if k % 512:
        return np.exp2(np.random.permutation(np.resize(levels, k // 32))).repeat(32)
    a = np.empty((k // 512, 16))
    for p in range(k // 512):
        a[p, :8] = np.random.permutation(np.resize(levels, 8))
        for g in range(8):
            far = levels[np.abs(levels - a[p, g]) >= 10]
            a[p, g + 8] = far[np.random.randint(len(far))]
    return np.exp2(a.ravel()).repeat(32)


BF16 = ml_dtypes.bfloat16


def bf(x):
    return np.asarray(x, np.float32).astype(BF16)


def f64(x):
    return np.asarray(x).astype(np.float64)


B, S, D, NH, HD, HID = 2, 128, 768, 4, 128, 16384


def setup_inputs():
    t = mx_kscale(HID)
    lengths = np.random.randint(S // 2, S + 1, size=B)
    tail = 0.05 + 0.45 * np.random.random_sample((B, S))
    mask = np.where(np.arange(S)[None, :] < lengths[:, None], 1.0, tail)
    h = np.random.standard_normal((NH, B, S, HD)) + 0.3 * np.random.standard_normal((NH, 1, 1, HD))
    return {"h_heads": bf(h),
            "attention_mask": bf(mask),
            "W1": bf(np.random.standard_normal((NH, HID, HD)) / np.sqrt(HD) * t[None, :, None]),
            "b1": bf(np.random.standard_normal((NH, HID)) * 0.2 * t[None, :]),
            "W2": bf(np.random.standard_normal((NH, HD, HID)) * 2.5 / np.sqrt(HID) / t[None, None, :])}


def reference(h_heads, attention_mask, W1, b1, W2):
    h = f64(h_heads)
    pre = h.reshape(NH, B * S, HD) @ f64(W1).transpose(0, 2, 1) + f64(b1)[:, None, :]
    hid = np.maximum(pre, 0.0)
    a = mxq(hid, 2, "e4m3") @ mxq(f64(W2), 2, "e4m3").transpose(0, 2, 1)
    with np.errstate(divide="ignore"):
        log_mask = np.log(f64(attention_mask))[None, :, :, None]
    a = a.reshape(NH, B, S, HD) + log_mask
    e = np.exp(a - a.max(axis=2, keepdims=True))
    w = e / e.sum(axis=2, keepdims=True)
    v = (h * w).sum(axis=2)
    return v.transpose(1, 0, 2).reshape(B, NH * HD)

@@ -1,0 +1,313 @@
+from contextlib import ExitStack
+
+import concourse.mybir as mybir
+from concourse.masks import make_identity
+
+BF16 = mybir.dt.bfloat16
+F32 = mybir.dt.float32
+U32 = mybir.dt.uint32
+U8 = mybir.dt.uint8
+FP8X4 = mybir.dt.float8_e4m3fn_x4
+ACT = mybir.ActivationFunctionType
+ALU = mybir.AluOpType
+AXIS = mybir.AxisListType
+
+P = 128
+HEADS = 4
+SENTENCES = 2
+TOKENS = 128
+FEAT = 128
+HID = 16384
+NTOK = SENTENCES * TOKENS
+
+PACK = 4
+K_PASS = P * PACK
+CHUNK = P
+
+STEP_PASSES = 2
+STEP_HID = STEP_PASSES * K_PASS
+STEP_CHUNKS = STEP_PASSES * PACK
+STEPS_PER_HEAD = HID // STEP_HID
+STEPS = HEADS * STEPS_PER_HEAD
+
+LOAD_STEPS = 2
+LOAD_HID = LOAD_STEPS * STEP_HID
+LOADS_PER_HEAD = HID // LOAD_HID
+LOADS = HEADS * LOADS_PER_HEAD
+LOADS_AHEAD = 3
+
+FLOPS = 2 * (2 * HEADS * NTOK * FEAT * HID)
+
+
+def tile_multiheadgeneralizedpooling_pa_k_kernel(
+    tc, h_heads, attention_mask, W1, b1, W2, out
+):
+    nc = tc.nc
+    with ExitStack() as ctx:
+        const = ctx.enter_context(tc.tile_pool(name="const", bufs=1))
+        raw = ctx.enter_context(tc.tile_pool(name="raw", bufs=LOADS_AHEAD + 1))
+        work = ctx.enter_context(tc.tile_pool(name="work", bufs=3))
+        codes = ctx.enter_context(tc.tile_pool(name="codes", bufs=6))
+        small = ctx.enter_context(tc.tile_pool(name="small", bufs=2))
+        psum = ctx.enter_context(tc.psum_pool(name="psum", bufs=1))
+        ctx.enter_context(tc.manual_schedule())
+
+        def load_weights(load):
+            head, part = divmod(load, LOADS_PER_HEAD)
+            units = slice(part * LOAD_HID, (part + 1) * LOAD_HID)
+            w1_raw = raw.tile([P, LOAD_HID // K_PASS, PACK * FEAT], BF16)
+            nc.sync.dma_start(
+                out=w1_raw[:],
+                in_=W1[head, units, :].rearrange("(g p t) d -> p g (t d)", p=P, t=PACK),
+            )
+            w2_raw = raw.tile([P, LOAD_HID], BF16)
+            nc.sync.dma_start(out=w2_raw[:], in_=W2[head, :, units])
+            return w1_raw, w2_raw
+
+        mask_all = const.tile([P, NTOK], BF16)
+        nc.scalar.dma_start(
+            out=mask_all[:], in_=attention_mask.rearrange("b s -> (b s)").partition_broadcast(P)
+        )
+        b_raw = const.tile([P, K_PASS], BF16)
+        nc.scalar.dma_start(out=b_raw[:], in_=b1.rearrange("i (r c) -> (i r) c", c=K_PASS))
+        h_raw = const.tile([P, HEADS * SENTENCES, FEAT], BF16)
+        nc.sync.dma_start(out=h_raw[:], in_=h_heads.rearrange("i b s d -> s (i b) d"))
+        raw_tiles = {}
+        for load in range(LOADS_AHEAD):
+            raw_tiles[load] = load_weights(load)
+
+        ident_bf = const.tile([P, P], BF16)
+        make_identity(nc, ident_bf[:])
+        ident_f32 = const.tile([P, P], F32)
+        make_identity(nc, ident_f32[:])
+
+        log_mask = const.tile([P, NTOK], F32)
+        nc.scalar.activation(out=log_mask[:], in_=mask_all[:], func=ACT.Ln)
+
+        h_bank = psum.tile([P, STEP_CHUNKS, P], BF16, tag="w1_bank", bufs=2)
+        for ib in range(HEADS * SENTENCES):
+            nc.tensor.transpose(h_bank[:, ib, :], h_raw[:, ib, :], ident_bf[:])
+        hT_bf = const.tile([P, HEADS * NTOK], BF16)
+        nc.vector.tensor_copy(out=hT_bf[:], in_=h_bank[:].rearrange("p c s -> p (c s)"))
+        hT_f32 = const.tile([P, HEADS * NTOK], F32)
+        nc.scalar.copy(out=hT_f32[:], in_=hT_bf[:])
+
+        b_bank = psum.tile([P, 2 * STEP_PASSES, P], F32, tag="w2_bank", bufs=1)
+        b_words = b_raw[:].bitcast(F32)
+        for u in range(2):
+            nc.tensor.transpose(b_bank[:, u, :], b_words[:, u::2], ident_f32[:])
+        bias = const.tile([P, HEADS * HID // CHUNK], F32)
+        nc.scalar.copy(
+            out=bias[:].rearrange("p (r u e) -> p r u e", u=2, e=2),
+            in_=b_bank[:].bitcast(BF16)[:, 0:2, :].rearrange("p u (r e) -> p r u e", e=2),
+        )
+
+        pooled = const.tile([P, P], F32)
+        nc.vector.memset(pooled[:], 0.0)
+
+        weight_banks = {}
+        w1T_tiles = {}
+        w2_grouped_tiles = {}
+        w2_mx = {}
+        plane_tiles = {}
+        hid_grouped_tiles = {}
+        hid_mx = {}
+        score_banks = {}
+        softmax_tiles = {}
+        exp_tiles = {}
+
+        def transpose_weights(step):
+            w1_raw, w2_raw = raw_tiles[step // LOAD_STEPS]
+            local = step % LOAD_STEPS
+            w1_bank = psum.tile([P, STEP_CHUNKS, P], BF16, tag="w1_bank", bufs=2)
+            for c in range(STEP_CHUNKS):
+                g, t = divmod(local * STEP_CHUNKS + c, PACK)
+                nc.tensor.transpose(
+                    w1_bank[:, c, :], w1_raw[:, g, t * FEAT : (t + 1) * FEAT], ident_bf[:]
+                )
+            w2_words = w2_raw[:].bitcast(F32)
+            w2_bank = psum.tile([P, 2 * STEP_PASSES, P], F32, tag="w2_bank", bufs=1)
+            for gu in range(2 * STEP_PASSES):
+                g, u = divmod(gu, 2)
+                first = (local * STEP_PASSES + g) * 2 * P
+                nc.tensor.transpose(
+                    w2_bank[:, gu, :], w2_words[:, first + u : first + 2 * P : 2], ident_f32[:]
+                )
+            weight_banks[step] = (w1_bank, w2_bank)
+
+        def empty_weight_banks(step):
+            w1_bank, w2_bank = weight_banks[step]
+            w2_grouped = work.tile([P, STEP_PASSES * FEAT * PACK], BF16, align_bytes=64)
+            w2_pairs = w2_grouped[:].bitcast(F32).rearrange("p (g d u) -> p g d u", d=FEAT, u=2)
+            w2_planes = w2_bank[:].rearrange("p (g u) d -> p g d u", u=2)
+            if step % 4 == 0:
+                nc.vector.tensor_copy(out=w2_pairs, in_=w2_planes)
+            else:
+                nc.scalar.copy(out=w2_pairs, in_=w2_planes)
+            w2_grouped_tiles[step] = w2_grouped
+            w1T = work.tile([P, STEP_CHUNKS, CHUNK], BF16)
+            nc.vector.tensor_copy(out=w1T[:], in_=w1_bank[:])
+            w1T_tiles[step] = w1T
+
+        def quantise_w2(step):
+            w2_codes = codes.tile([P, STEP_PASSES * FEAT], U32, align_bytes=64)
+            w2_scales = codes.tile([P, STEP_PASSES * FEAT], U8, align_bytes=64)
+            nc.vector.quantize_mx(
+                out=w2_codes[:].bitcast(FP8X4), scales=w2_scales[:], in_=w2_grouped_tiles[step][:]
+            )
+            w2_mx[step] = (w2_codes, w2_scales)
+
+        def hidden_layer(step):
+            head = step // STEPS_PER_HEAD
+            w1T = w1T_tiles[step]
+            planes = work.tile([P, PACK, STEP_PASSES * NTOK], BF16)
+            for pair in range(STEP_CHUNKS // 2):
+                hid_bank = psum.tile([P, 2, NTOK], F32, tag="hid_bank", bufs=4)
+                for half in range(2):
+                    nc.tensor.matmul(
+                        hid_bank[:, half, :],
+                        lhsT=w1T[:, 2 * pair + half, :],
+                        rhs=hT_bf[:, head * NTOK : (head + 1) * NTOK],
+                        start=True,
+                        stop=True,
+                    )
+                for half in range(2):
+                    chunk = 2 * pair + half
+                    g, t = divmod(chunk, PACK)
+                    column = step * STEP_CHUNKS + chunk
+                    nc.scalar.activation(
+                        out=planes[:, t, g * NTOK : (g + 1) * NTOK],
+                        in_=hid_bank[:, half, :],
+                        func=ACT.Relu,
+                        bias=bias[:, column : column + 1],
+                        scale=1.0,
+                    )
+            plane_tiles[step] = planes
+
+        def group_hidden(step):
+            planes = plane_tiles[step]
+            hid_grouped = work.tile([P, STEP_PASSES * NTOK * PACK], BF16, align_bytes=64)
+            nc.vector.tensor_copy(
+                out=hid_grouped[:].rearrange("p (c i t) -> p c t i", i=4, t=PACK),
+                in_=planes[:].rearrange("p t (c i) -> p c t i", i=4),
+            )
+            hid_grouped_tiles[step] = hid_grouped
+
+        def quantise_hidden(step):
+            hid_codes = codes.tile([P, STEP_PASSES * NTOK], U32, align_bytes=64)
+            hid_scales = codes.tile([P, STEP_PASSES * NTOK], U8, align_bytes=64)
+            nc.vector.quantize_mx(
+                out=hid_codes[:].bitcast(FP8X4),
+                scales=hid_scales[:],
+                in_=hid_grouped_tiles[step][:],
+            )
+            hid_mx[step] = (hid_codes, hid_scales)
+
+        def second_layer(step):
+            head, part = divmod(step, STEPS_PER_HEAD)
+            if part == 0:
+                scores = psum.tile([P, NTOK], F32, tag="scores", bufs=1)
+                score_banks[head] = scores
+            scores = score_banks[head]
+            w2_codes, w2_scales = w2_mx[step]
+            hid_codes, hid_scales = hid_mx[step]
+            for g in range(STEP_PASSES):
+                feats = slice(g * FEAT, (g + 1) * FEAT)
+                toks = slice(g * NTOK, (g + 1) * NTOK)
+                nc.tensor.matmul_mx(
+                    out=scores[:],
+                    lhsT=w2_codes[:, feats].bitcast(FP8X4),
+                    lhsT_scale=w2_scales[:, feats],
+                    rhs=hid_codes[:, toks].bitcast(FP8X4),
+                    rhs_scale=hid_scales[:, toks],
+                    start=(part == 0 and g == 0),
+                    stop=(part == STEPS_PER_HEAD - 1 and g == STEP_PASSES - 1),
+                )
+
+        def softmax_shift(head):
+            a = small.tile([P, SENTENCES, TOKENS], F32)
+            nc.vector.tensor_tensor(
+                out=a[:].rearrange("p b s -> p (b s)"),
+                in0=score_banks[head][:],
+                in1=log_mask[:],
+                op=ALU.add,
+            )
+            a_max = small.tile([P, SENTENCES], F32)
+            nc.vector.tensor_reduce(out=a_max[:], in_=a[:], axis=AXIS.X, op=ALU.max)
+            neg_max = small.tile([P, SENTENCES], F32)
+            nc.vector.tensor_scalar_mul(out=neg_max[:], in0=a_max[:], scalar1=-1.0)
+            softmax_tiles[head] = (a, neg_max)
+
+        def softmax_exp(head):
+            a, neg_max = softmax_tiles[head]
+            e = small.tile([P, SENTENCES, TOKENS], F32)
+            e_sum = small.tile([P, SENTENCES], F32)
+            for b in range(SENTENCES):
+                nc.scalar.activation(
+                    out=e[:, b, :],
+                    in_=a[:, b, :],
+                    func=ACT.Exp,
+                    bias=neg_max[:, b : b + 1],
+                    scale=1.0,
+                    accum_out=e_sum[:, b : b + 1],
+                )
+            exp_tiles[head] = (e, e_sum)
+
+        def weighted_sum(head):
+            e, e_sum = exp_tiles[head]
+            he = small.tile([P, SENTENCES, TOKENS], F32)
+            nc.vector.tensor_tensor(
+                out=he[:].rearrange("p b s -> p (b s)"),
+                in0=e[:].rearrange("p b s -> p (b s)"),
+                in1=hT_f32[:, head * NTOK : (head + 1) * NTOK],
+                op=ALU.mult,
+            )
+            he_sum = small.tile([P, SENTENCES], F32)
+            nc.vector.tensor_reduce(out=he_sum[:], in_=he[:], axis=AXIS.X, op=ALU.add)
+            inv_sum = small.tile([P, SENTENCES], F32)
+            nc.vector.reciprocal(out=inv_sum[:], in_=e_sum[:])
+            nc.vector.tensor_tensor(
+                out=pooled[:, 0 : SENTENCES * HEADS].rearrange("p (b i) -> p b i", i=HEADS)[:, :, head],
+                in0=he_sum[:],
+                in1=inv_sum[:],
+                op=ALU.mult,
+            )
+
+        def is_step(step):
+            return 0 <= step < STEPS
+
+        def ends_a_head(step):
+            return is_step(step) and step % STEPS_PER_HEAD == STEPS_PER_HEAD - 1
+
+        for r in range(-1, STEPS + 4):
+            if is_step(r + 1):
+                load = (r + 1) // LOAD_STEPS + LOADS_AHEAD
+                if (r + 1) % LOAD_STEPS == 0 and load < LOADS:
+                    raw_tiles[load] = load_weights(load)
+                transpose_weights(r + 1)
+            if is_step(r - 3):
+                second_layer(r - 3)
+            if ends_a_head(r - 3):
+                softmax_shift((r - 3) // STEPS_PER_HEAD)
+            if is_step(r + 1):
+                empty_weight_banks(r + 1)
+            if is_step(r):
+                hidden_layer(r)
+            if ends_a_head(r - 3):
+                softmax_exp((r - 3) // STEPS_PER_HEAD)
+            if is_step(r - 1):
+                group_hidden(r - 1)
+            if is_step(r + 1):
+                quantise_w2(r + 1)
+            if is_step(r - 1):
+                quantise_hidden(r - 1)
+            if ends_a_head(r - 4):
+                weighted_sum((r - 4) // STEPS_PER_HEAD)
+
+        out_bank = psum.tile([P, 2 * STEP_PASSES, P], F32, tag="w2_bank", bufs=1)
+        nc.tensor.transpose(out_bank[:, 0, :], pooled[:], ident_f32[:])
+        out_rows = small.tile([P, FEAT], F32)
+        nc.vector.tensor_copy(out=out_rows[:], in_=out_bank[:, 0, :])
+        nc.sync.dma_start(
+            out=out.rearrange("b (i d) -> (b i) d", d=FEAT), in_=out_rows[0 : SENTENCES * HEADS, :]
+        )

@@ -157,11 +157,14 @@ def tile_multiheadgeneralizedpooling_pa_k_kernel(
             )
             w2_mx[step] = (w2_codes, w2_scales)
 
-        def hidden_layer(step):
+        def hidden_layer(step, pairs):
             head = step // STEPS_PER_HEAD
             w1T = w1T_tiles[step]
-            planes = work.tile([P, PACK, STEP_PASSES * NTOK], BF16)
-            for pair in range(STEP_CHUNKS // 2):
+            if step not in plane_tiles:
+                planes = work.tile([P, PACK, STEP_PASSES * NTOK], BF16)
+                plane_tiles[step] = planes
+            planes = plane_tiles[step]
+            for pair in pairs:
                 hid_bank = psum.tile([P, 2, NTOK], F32, tag="hid_bank", bufs=4)
                 for half in range(2):
                     nc.tensor.matmul(
@@ -182,7 +185,6 @@ def tile_multiheadgeneralizedpooling_pa_k_kernel(
                         bias=bias[:, column : column + 1],
                         scale=1.0,
                     )
-            plane_tiles[step] = planes
 
         def group_hidden(step):
             planes = plane_tiles[step]
@@ -285,14 +287,16 @@ def tile_multiheadgeneralizedpooling_pa_k_kernel(
                 if (r + 1) % LOAD_STEPS == 0 and load < LOADS:
                     raw_tiles[load] = load_weights(load)
                 transpose_weights(r + 1)
+            if is_step(r + 1):
+                empty_weight_banks(r + 1)
+            if is_step(r):
+                hidden_layer(r, range(STEP_CHUNKS // 4))
             if is_step(r - 3):
                 second_layer(r - 3)
             if ends_a_head(r - 3):
                 softmax_shift((r - 3) // STEPS_PER_HEAD)
-            if is_step(r + 1):
-                empty_weight_banks(r + 1)
             if is_step(r):
-                hidden_layer(r)
+                hidden_layer(r, range(STEP_CHUNKS // 4, STEP_CHUNKS // 2))
             if ends_a_head(r - 3):
                 softmax_exp((r - 3) // STEPS_PER_HEAD)
             if is_step(r - 1):

@@ -140,13 +140,10 @@ def tile_multiheadgeneralizedpooling_pa_k_kernel(
             w2_grouped = work.tile([P, STEP_PASSES * FEAT * PACK], BF16, align_bytes=64)
             w2_pairs = w2_grouped[:].bitcast(F32).rearrange("p (g d u) -> p g d u", d=FEAT, u=2)
             w2_planes = w2_bank[:].rearrange("p (g u) d -> p g d u", u=2)
-            if step % 4 == 0:
-                nc.vector.tensor_copy(out=w2_pairs, in_=w2_planes)
-            else:
-                nc.scalar.copy(out=w2_pairs, in_=w2_planes)
+            nc.scalar.copy(out=w2_pairs, in_=w2_planes)
             w2_grouped_tiles[step] = w2_grouped
             w1T = work.tile([P, STEP_CHUNKS, CHUNK], BF16)
-            nc.vector.tensor_copy(out=w1T[:], in_=w1_bank[:])
+            nc.scalar.copy(out=w1T[:], in_=w1_bank[:])
             w1T_tiles[step] = w1T
 
         def quantise_w2(step):
@@ -157,43 +154,72 @@ def tile_multiheadgeneralizedpooling_pa_k_kernel(
             )
             w2_mx[step] = (w2_codes, w2_scales)
 
-        def hidden_layer(step, pairs):
+        def direct_tokens(step):
+            return TOKENS * (2 if step % 3 == 2 else 1)
+
+        def first_matmul(step, out_ap, chunk, tokens):
             head = step // STEPS_PER_HEAD
-            w1T = w1T_tiles[step]
-            if step not in plane_tiles:
-                planes = work.tile([P, PACK, STEP_PASSES * NTOK], BF16)
-                plane_tiles[step] = planes
+            nc.tensor.matmul(
+                out_ap,
+                lhsT=w1T_tiles[step][:, chunk, :],
+                rhs=hT_bf[:, head * NTOK + tokens.start : head * NTOK + tokens.stop],
+                start=True,
+                stop=True,
+            )
+
+        def open_hidden(step):
+            planes = work.tile([P, PACK, STEP_PASSES * NTOK], BF16)
+            plane_tiles[step] = planes
+            hid_grouped = work.tile([P, STEP_PASSES * NTOK * PACK], BF16, align_bytes=64)
+            hid_grouped_tiles[step] = hid_grouped
+
+        def hidden_direct(step):
+            column = step * STEP_CHUNKS
+            for b in range(direct_tokens(step) // TOKENS):
+                bank = psum.tile([P, PACK, TOKENS], F32, tag="hid_bank", bufs=4)
+                for t in range(PACK):
+                    first_matmul(step, bank[:, t, :], t, slice(b * TOKENS, (b + 1) * TOKENS))
+                words = hid_grouped_tiles[step][:, b * TOKENS * PACK : (b + 1) * TOKENS * PACK]
+                nc.vector.tensor_tensor(
+                    out=words.rearrange("p (s t) -> p s t", t=PACK),
+                    in0=bank[:].rearrange("p t s -> p s t"),
+                    in1=bias[:, column : column + PACK].unsqueeze(1).to_broadcast([P, TOKENS, PACK]),
+                    op=ALU.add,
+                )
+
+        def relu_direct(step):
+            words = hid_grouped_tiles[step][:, 0 : direct_tokens(step) * PACK]
+            nc.vector.tensor_scalar_max(out=words, in0=words, scalar1=0.0)
+
+        def hidden_planes(step, g):
             planes = plane_tiles[step]
-            for pair in pairs:
-                hid_bank = psum.tile([P, 2, NTOK], F32, tag="hid_bank", bufs=4)
-                for half in range(2):
-                    nc.tensor.matmul(
-                        hid_bank[:, half, :],
-                        lhsT=w1T[:, 2 * pair + half, :],
-                        rhs=hT_bf[:, head * NTOK : (head + 1) * NTOK],
-                        start=True,
-                        stop=True,
-                    )
-                for half in range(2):
-                    chunk = 2 * pair + half
-                    g, t = divmod(chunk, PACK)
-                    column = step * STEP_CHUNKS + chunk
-                    nc.scalar.activation(
-                        out=planes[:, t, g * NTOK : (g + 1) * NTOK],
-                        in_=hid_bank[:, half, :],
-                        func=ACT.Relu,
-                        bias=bias[:, column : column + 1],
-                        scale=1.0,
-                    )
+            first = direct_tokens(step) if g == 0 else 0
+            width = NTOK - first
+            per_bank = 2 * NTOK // width if width else 0
+            for c in range(PACK if width else 0):
+                if c % per_bank == 0:
+                    bank = psum.tile([P, per_bank, width], F32, tag="hid_bank", bufs=4)
+                    for half in range(per_bank):
+                        first_matmul(
+                            step, bank[:, half, :], g * PACK + c + half, slice(first, NTOK)
+                        )
+                column = step * STEP_CHUNKS + g * PACK + c
+                nc.scalar.activation(
+                    out=planes[:, c, g * NTOK + first : (g + 1) * NTOK],
+                    in_=bank[:, c % per_bank, :],
+                    func=ACT.Relu,
+                    bias=bias[:, column : column + 1],
+                    scale=1.0,
+                )
 
         def group_hidden(step):
-            planes = plane_tiles[step]
-            hid_grouped = work.tile([P, STEP_PASSES * NTOK * PACK], BF16, align_bytes=64)
+            first = direct_tokens(step)
             nc.vector.tensor_copy(
-                out=hid_grouped[:].rearrange("p (c i t) -> p c t i", i=4, t=PACK),
-                in_=planes[:].rearrange("p t (c i) -> p c t i", i=4),
+                out=hid_grouped_tiles[step][:, first * PACK :].rearrange(
+                    "p (c i t) -> p c t i", i=4, t=PACK
+                ),
+                in_=plane_tiles[step][:, :, first:].rearrange("p t (c i) -> p c t i", i=4),
             )
-            hid_grouped_tiles[step] = hid_grouped
 
         def quantise_hidden(step):
             hid_codes = codes.tile([P, STEP_PASSES * NTOK], U32, align_bytes=64)
@@ -289,20 +315,24 @@ def tile_multiheadgeneralizedpooling_pa_k_kernel(
                 transpose_weights(r + 1)
             if is_step(r + 1):
                 empty_weight_banks(r + 1)
+            if is_step(r - 1):
+                group_hidden(r - 1)
             if is_step(r):
-                hidden_layer(r, range(STEP_CHUNKS // 4))
+                open_hidden(r)
+                hidden_direct(r)
+                hidden_planes(r, 0)
             if is_step(r - 3):
                 second_layer(r - 3)
             if ends_a_head(r - 3):
                 softmax_shift((r - 3) // STEPS_PER_HEAD)
             if is_step(r):
-                hidden_layer(r, range(STEP_CHUNKS // 4, STEP_CHUNKS // 2))
+                hidden_planes(r, 1)
             if ends_a_head(r - 3):
                 softmax_exp((r - 3) // STEPS_PER_HEAD)
-            if is_step(r - 1):
-                group_hidden(r - 1)
             if is_step(r + 1):
                 quantise_w2(r + 1)
+            if is_step(r):
+                relu_direct(r)
             if is_step(r - 1):
                 quantise_hidden(r - 1)
             if ends_a_head(r - 4):

@@ -30,11 +30,9 @@ STEP_CHUNKS = STEP_PASSES * PACK
 STEPS_PER_HEAD = HID // STEP_HID
 STEPS = HEADS * STEPS_PER_HEAD
 
-LOAD_STEPS = 2
-LOAD_HID = LOAD_STEPS * STEP_HID
-LOADS_PER_HEAD = HID // LOAD_HID
-LOADS = HEADS * LOADS_PER_HEAD
-LOADS_AHEAD = 3
+LOADS_AHEAD = 6
+
+REST_ROUND = 3
 
 FLOPS = 2 * (2 * HEADS * NTOK * FEAT * HID)
 
@@ -45,62 +43,80 @@ def tile_multiheadgeneralizedpooling_pa_k_kernel(
     nc = tc.nc
     with ExitStack() as ctx:
         const = ctx.enter_context(tc.tile_pool(name="const", bufs=1))
-        raw = ctx.enter_context(tc.tile_pool(name="raw", bufs=LOADS_AHEAD + 1))
+        raw = ctx.enter_context(tc.tile_pool(name="raw", bufs=LOADS_AHEAD + 2))
         work = ctx.enter_context(tc.tile_pool(name="work", bufs=3))
         codes = ctx.enter_context(tc.tile_pool(name="codes", bufs=6))
         small = ctx.enter_context(tc.tile_pool(name="small", bufs=2))
         psum = ctx.enter_context(tc.psum_pool(name="psum", bufs=1))
         ctx.enter_context(tc.manual_schedule())
 
-        def load_weights(load):
-            head, part = divmod(load, LOADS_PER_HEAD)
-            units = slice(part * LOAD_HID, (part + 1) * LOAD_HID)
-            w1_raw = raw.tile([P, LOAD_HID // K_PASS, PACK * FEAT], BF16)
+        def load_weights(step):
+            head, part = divmod(step, STEPS_PER_HEAD)
+            units = slice(part * STEP_HID, (part + 1) * STEP_HID)
+            w1_raw = raw.tile([P, STEP_PASSES, PACK * FEAT], BF16)
             nc.sync.dma_start(
                 out=w1_raw[:],
                 in_=W1[head, units, :].rearrange("(g p t) d -> p g (t d)", p=P, t=PACK),
             )
-            w2_raw = raw.tile([P, LOAD_HID], BF16)
+            w2_raw = raw.tile([P, STEP_HID], BF16)
             nc.sync.dma_start(out=w2_raw[:], in_=W2[head, :, units])
             return w1_raw, w2_raw
 
-        mask_all = const.tile([P, NTOK], BF16)
+        mask_row = const.tile([P, NTOK], BF16)
+        nc.vector.memset(mask_row[:], 0.0)
         nc.scalar.dma_start(
-            out=mask_all[:], in_=attention_mask.rearrange("b s -> (b s)").partition_broadcast(P)
+            out=mask_row[0:1, :], in_=attention_mask.rearrange("b s -> (b s)").unsqueeze(0)
         )
+        h_view = h_heads.rearrange("i b s d -> s (i b) d")
+        h_raw = const.tile([P, SENTENCES, FEAT], BF16)
+        nc.sync.dma_start(out=h_raw[:], in_=h_view[:, 0:SENTENCES, :])
         b_raw = const.tile([P, K_PASS], BF16)
-        nc.scalar.dma_start(out=b_raw[:], in_=b1.rearrange("i (r c) -> (i r) c", c=K_PASS))
-        h_raw = const.tile([P, HEADS * SENTENCES, FEAT], BF16)
-        nc.sync.dma_start(out=h_raw[:], in_=h_heads.rearrange("i b s d -> s (i b) d"))
+        nc.sync.dma_start(out=b_raw[:], in_=b1.rearrange("i (r c) -> (i r) c", c=K_PASS))
         raw_tiles = {}
-        for load in range(LOADS_AHEAD):
-            raw_tiles[load] = load_weights(load)
+        for step in range(2):
+            raw_tiles[step] = load_weights(step)
+        h_rest_raw = const.tile([P, (HEADS - 1) * SENTENCES, FEAT], BF16)
+        nc.sync.dma_start(out=h_rest_raw[:], in_=h_view[:, SENTENCES:, :])
+        for step in range(2, LOADS_AHEAD):
+            raw_tiles[step] = load_weights(step)
 
         ident_bf = const.tile([P, P], BF16)
         make_identity(nc, ident_bf[:])
         ident_f32 = const.tile([P, P], F32)
         make_identity(nc, ident_f32[:])
+        ones = const.tile([P, P], BF16)
+        nc.vector.memset(ones[:], 1.0)
 
-        log_mask = const.tile([P, NTOK], F32)
-        nc.scalar.activation(out=log_mask[:], in_=mask_all[:], func=ACT.Ln)
-
-        h_bank = psum.tile([P, STEP_CHUNKS, P], BF16, tag="w1_bank", bufs=2)
-        for ib in range(HEADS * SENTENCES):
-            nc.tensor.transpose(h_bank[:, ib, :], h_raw[:, ib, :], ident_bf[:])
         hT_bf = const.tile([P, HEADS * NTOK], BF16)
-        nc.vector.tensor_copy(out=hT_bf[:], in_=h_bank[:].rearrange("p c s -> p (c s)"))
         hT_f32 = const.tile([P, HEADS * NTOK], F32)
-        nc.scalar.copy(out=hT_f32[:], in_=hT_bf[:])
 
-        b_bank = psum.tile([P, 2 * STEP_PASSES, P], F32, tag="w2_bank", bufs=1)
+        def transpose_h(source, count, first):
+            bank = psum.tile([P, STEP_CHUNKS, P], BF16, tag="w1_bank", bufs=2)
+            for ib in range(count):
+                nc.tensor.transpose(bank[:, ib, :], source[:, ib, :], ident_bf[:])
+            nc.vector.tensor_copy(
+                out=hT_bf[:, first * P : (first + count) * P],
+                in_=bank[:, 0:count, :].rearrange("p c s -> p (c s)"),
+            )
+
+        transpose_h(h_raw, SENTENCES, 0)
+
+        b_bank = psum.tile([P, 2 * STEP_PASSES, P], F32, tag="hid_bank", bufs=4)
         b_words = b_raw[:].bitcast(F32)
         for u in range(2):
             nc.tensor.transpose(b_bank[:, u, :], b_words[:, u::2], ident_f32[:])
         bias = const.tile([P, HEADS * HID // CHUNK], F32)
-        nc.scalar.copy(
+        nc.vector.tensor_copy(
             out=bias[:].rearrange("p (r u e) -> p r u e", u=2, e=2),
             in_=b_bank[:].bitcast(BF16)[:, 0:2, :].rearrange("p u (r e) -> p r u e", e=2),
         )
+
+        mask_bank = psum.tile([P, NTOK], F32, tag="hid_bank", bufs=4)
+        nc.tensor.matmul(mask_bank[:], lhsT=ones[:], rhs=mask_row[:], start=True, stop=True)
+        log_mask = const.tile([P, NTOK], F32)
+        nc.scalar.activation(out=log_mask[:], in_=mask_bank[:], func=ACT.Ln)
+        exp_first = const.tile([P, 1], F32)
+        nc.scalar.activation(out=exp_first[:], in_=log_mask[:, 0:1], func=ACT.Exp)
 
         pooled = const.tile([P, P], F32)
         nc.vector.memset(pooled[:], 0.0)
@@ -117,11 +133,10 @@ def tile_multiheadgeneralizedpooling_pa_k_kernel(
         exp_tiles = {}
 
         def transpose_weights(step):
-            w1_raw, w2_raw = raw_tiles[step // LOAD_STEPS]
-            local = step % LOAD_STEPS
+            w1_raw, w2_raw = raw_tiles[step]
             w1_bank = psum.tile([P, STEP_CHUNKS, P], BF16, tag="w1_bank", bufs=2)
             for c in range(STEP_CHUNKS):
-                g, t = divmod(local * STEP_CHUNKS + c, PACK)
+                g, t = divmod(c, PACK)
                 nc.tensor.transpose(
                     w1_bank[:, c, :], w1_raw[:, g, t * FEAT : (t + 1) * FEAT], ident_bf[:]
                 )
@@ -129,7 +144,7 @@ def tile_multiheadgeneralizedpooling_pa_k_kernel(
             w2_bank = psum.tile([P, 2 * STEP_PASSES, P], F32, tag="w2_bank", bufs=1)
             for gu in range(2 * STEP_PASSES):
                 g, u = divmod(gu, 2)
-                first = (local * STEP_PASSES + g) * 2 * P
+                first = g * 2 * P
                 nc.tensor.transpose(
                     w2_bank[:, gu, :], w2_words[:, first + u : first + 2 * P : 2], ident_f32[:]
                 )
@@ -253,30 +268,30 @@ def tile_multiheadgeneralizedpooling_pa_k_kernel(
                 )
 
         def softmax_shift(head):
-            a = small.tile([P, SENTENCES, TOKENS], F32)
-            nc.vector.tensor_tensor(
-                out=a[:].rearrange("p b s -> p (b s)"),
+            neg_a = small.tile([P, SENTENCES, TOKENS], F32)
+            nc.vector.scalar_tensor_tensor(
+                out=neg_a[:].rearrange("p b s -> p (b s)"),
                 in0=score_banks[head][:],
+                scalar=-1.0,
                 in1=log_mask[:],
-                op=ALU.add,
+                op0=ALU.mult,
+                op1=ALU.subtract,
             )
-            a_max = small.tile([P, SENTENCES], F32)
-            nc.vector.tensor_reduce(out=a_max[:], in_=a[:], axis=AXIS.X, op=ALU.max)
             neg_max = small.tile([P, SENTENCES], F32)
-            nc.vector.tensor_scalar_mul(out=neg_max[:], in0=a_max[:], scalar1=-1.0)
-            softmax_tiles[head] = (a, neg_max)
+            nc.vector.tensor_reduce(out=neg_max[:], in_=neg_a[:], axis=AXIS.X, op=ALU.min)
+            softmax_tiles[head] = (neg_a, neg_max)
 
         def softmax_exp(head):
-            a, neg_max = softmax_tiles[head]
+            neg_a, neg_max = softmax_tiles[head]
             e = small.tile([P, SENTENCES, TOKENS], F32)
             e_sum = small.tile([P, SENTENCES], F32)
             for b in range(SENTENCES):
                 nc.scalar.activation(
                     out=e[:, b, :],
-                    in_=a[:, b, :],
+                    in_=neg_a[:, b, :],
                     func=ACT.Exp,
                     bias=neg_max[:, b : b + 1],
-                    scale=1.0,
+                    scale=-1.0,
                     accum_out=e_sum[:, b : b + 1],
                 )
             exp_tiles[head] = (e, e_sum)
@@ -308,10 +323,14 @@ def tile_multiheadgeneralizedpooling_pa_k_kernel(
             return is_step(step) and step % STEPS_PER_HEAD == STEPS_PER_HEAD - 1
 
         for r in range(-1, STEPS + 4):
+            if r == REST_ROUND:
+                transpose_h(h_rest_raw, (HEADS - 1) * SENTENCES, SENTENCES)
+                nc.gpsimd.tensor_scalar(
+                    out=hT_f32[:], in0=hT_bf[:], scalar1=1.0, scalar2=0.0, op0=ALU.mult, op1=ALU.add
+                )
             if is_step(r + 1):
-                load = (r + 1) // LOAD_STEPS + LOADS_AHEAD
-                if (r + 1) % LOAD_STEPS == 0 and load < LOADS:
-                    raw_tiles[load] = load_weights(load)
+                if is_step(r + 1 + LOADS_AHEAD):
+                    raw_tiles[r + 1 + LOADS_AHEAD] = load_weights(r + 1 + LOADS_AHEAD)
                 transpose_weights(r + 1)
             if is_step(r + 1):
                 empty_weight_banks(r + 1)

@@ -111,6 +111,14 @@ def tile_multiheadgeneralizedpooling_pa_k_kernel(
             in_=b_bank[:].bitcast(BF16)[:, 0:2, :].rearrange("p u (r e) -> p r u e", e=2),
         )
 
+        rows_bank = psum.tile([P, 2 * STEP_PASSES, P], F32, tag="hid_bank", bufs=4)
+        for block in range(HEADS * HID // CHUNK // P):
+            nc.tensor.transpose(
+                rows_bank[:, block, :], bias[:, block * P : (block + 1) * P], ident_f32[:]
+            )
+        bias_rows = const.tile([P, 2 * STEP_PASSES, P], BF16)
+        nc.vector.tensor_copy(out=bias_rows[:], in_=rows_bank[:])
+
         mask_bank = psum.tile([P, NTOK], F32, tag="hid_bank", bufs=4)
         nc.tensor.matmul(mask_bank[:], lhsT=ones[:], rhs=mask_row[:], start=True, stop=True)
         log_mask = const.tile([P, NTOK], F32)
@@ -169,17 +177,25 @@ def tile_multiheadgeneralizedpooling_pa_k_kernel(
             )
             w2_mx[step] = (w2_codes, w2_scales)
 
-        def direct_tokens(step):
-            return TOKENS * (2 if step % 3 == 2 else 1)
+        def second_sentence(step):
+            if step % 2 == 1:
+                return "vector"
+            return "planes" if step % 8 == 6 else "bias matmul"
 
-        def first_matmul(step, out_ap, chunk, tokens):
+        def direct_tokens(step):
+            return NTOK if second_sentence(step) == "vector" else TOKENS
+
+        def plane_columns(step):
+            return TOKENS if second_sentence(step) == "planes" else NTOK
+
+        def first_matmul(step, out_ap, chunk, tokens, alone=True, last=True):
             head = step // STEPS_PER_HEAD
             nc.tensor.matmul(
                 out_ap,
                 lhsT=w1T_tiles[step][:, chunk, :],
                 rhs=hT_bf[:, head * NTOK + tokens.start : head * NTOK + tokens.stop],
-                start=True,
-                stop=True,
+                start=alone,
+                stop=last,
             )
 
         def open_hidden(step):
@@ -202,13 +218,36 @@ def tile_multiheadgeneralizedpooling_pa_k_kernel(
                     op=ALU.add,
                 )
 
+        def hidden_biased(step):
+            if second_sentence(step) != "bias matmul":
+                return
+            bank = psum.tile([P, PACK, TOKENS], F32, tag="hid_bank", bufs=4)
+            block, row = divmod(step * STEP_CHUNKS, P)
+            nc.tensor.matmul(
+                bank[:],
+                lhsT=bias_rows[:, block, :],
+                rhs=ident_bf[:, row : row + PACK].unsqueeze(2).to_broadcast([P, PACK, TOKENS]),
+                start=True,
+                stop=False,
+            )
+            for t in range(PACK):
+                first_matmul(
+                    step, bank[:, t, :], t, slice(TOKENS, NTOK), alone=False, last=t == PACK - 1
+                )
+            words = hid_grouped_tiles[step][:, TOKENS * PACK : NTOK * PACK]
+            nc.scalar.activation(
+                out=words.rearrange("p (s t) -> p s t", t=PACK),
+                in_=bank[:].rearrange("p t s -> p s t"),
+                func=ACT.Relu,
+            )
+
         def relu_direct(step):
             words = hid_grouped_tiles[step][:, 0 : direct_tokens(step) * PACK]
             nc.vector.tensor_scalar_max(out=words, in0=words, scalar1=0.0)
 
         def hidden_planes(step, g):
             planes = plane_tiles[step]
-            first = direct_tokens(step) if g == 0 else 0
+            first = plane_columns(step) if g == 0 else 0
             width = NTOK - first
             per_bank = 2 * NTOK // width if width else 0
             for c in range(PACK if width else 0):
@@ -228,7 +267,7 @@ def tile_multiheadgeneralizedpooling_pa_k_kernel(
                 )
 
         def group_hidden(step):
-            first = direct_tokens(step)
+            first = plane_columns(step)
             nc.vector.tensor_copy(
                 out=hid_grouped_tiles[step][:, first * PACK :].rearrange(
                     "p (c i t) -> p c t i", i=4, t=PACK
@@ -334,11 +373,10 @@ def tile_multiheadgeneralizedpooling_pa_k_kernel(
                 transpose_weights(r + 1)
             if is_step(r + 1):
                 empty_weight_banks(r + 1)
-            if is_step(r - 1):
-                group_hidden(r - 1)
             if is_step(r):
                 open_hidden(r)
                 hidden_direct(r)
+                hidden_biased(r)
                 hidden_planes(r, 0)
             if is_step(r - 3):
                 second_layer(r - 3)
@@ -348,6 +386,8 @@ def tile_multiheadgeneralizedpooling_pa_k_kernel(
                 hidden_planes(r, 1)
             if ends_a_head(r - 3):
                 softmax_exp((r - 3) // STEPS_PER_HEAD)
+            if is_step(r - 1):
+                group_hidden(r - 1)
             if is_step(r + 1):
                 quantise_w2(r + 1)
             if is_step(r):

@@ -63,18 +63,17 @@ def tile_multiheadgeneralizedpooling_pa_k_kernel(
             return w1_raw, w2_raw
 
         mask_row = const.tile([P, NTOK], BF16)
-        nc.vector.memset(mask_row[:], 0.0)
+        nc.gpsimd.memset(mask_row[:], 0.0)
         nc.scalar.dma_start(
             out=mask_row[0:1, :], in_=attention_mask.rearrange("b s -> (b s)").unsqueeze(0)
         )
+        raw_tiles = {0: load_weights(0)}
         h_view = h_heads.rearrange("i b s d -> s (i b) d")
         h_raw = const.tile([P, SENTENCES, FEAT], BF16)
         nc.sync.dma_start(out=h_raw[:], in_=h_view[:, 0:SENTENCES, :])
         b_raw = const.tile([P, K_PASS], BF16)
         nc.sync.dma_start(out=b_raw[:], in_=b1.rearrange("i (r c) -> (i r) c", c=K_PASS))
-        raw_tiles = {}
-        for step in range(2):
-            raw_tiles[step] = load_weights(step)
+        raw_tiles[1] = load_weights(1)
         h_rest_raw = const.tile([P, (HEADS - 1) * SENTENCES, FEAT], BF16)
         nc.sync.dma_start(out=h_rest_raw[:], in_=h_view[:, SENTENCES:, :])
         for step in range(2, LOADS_AHEAD):
@@ -87,6 +86,13 @@ def tile_multiheadgeneralizedpooling_pa_k_kernel(
         ones = const.tile([P, P], BF16)
         nc.vector.memset(ones[:], 1.0)
 
+        mask_bank = psum.tile([P, NTOK], F32, tag="hid_bank", bufs=4)
+        nc.tensor.matmul(mask_bank[:], lhsT=ones[:], rhs=mask_row[:], start=True, stop=True)
+        log_mask = const.tile([P, NTOK], F32)
+        nc.scalar.activation(out=log_mask[:], in_=mask_bank[:], func=ACT.Ln)
+        exp_first = const.tile([P, 1], F32)
+        nc.scalar.activation(out=exp_first[:], in_=log_mask[:, 0:1], func=ACT.Exp)
+
         hT_bf = const.tile([P, HEADS * NTOK], BF16)
         hT_f32 = const.tile([P, HEADS * NTOK], F32)
 
@@ -98,33 +104,6 @@ def tile_multiheadgeneralizedpooling_pa_k_kernel(
                 out=hT_bf[:, first * P : (first + count) * P],
                 in_=bank[:, 0:count, :].rearrange("p c s -> p (c s)"),
             )
-
-        transpose_h(h_raw, SENTENCES, 0)
-
-        b_bank = psum.tile([P, 2 * STEP_PASSES, P], F32, tag="hid_bank", bufs=4)
-        b_words = b_raw[:].bitcast(F32)
-        for u in range(2):
-            nc.tensor.transpose(b_bank[:, u, :], b_words[:, u::2], ident_f32[:])
-        bias = const.tile([P, HEADS * HID // CHUNK], F32)
-        nc.vector.tensor_copy(
-            out=bias[:].rearrange("p (r u e) -> p r u e", u=2, e=2),
-            in_=b_bank[:].bitcast(BF16)[:, 0:2, :].rearrange("p u (r e) -> p r u e", e=2),
-        )
-
-        rows_bank = psum.tile([P, 2 * STEP_PASSES, P], F32, tag="hid_bank", bufs=4)
-        for block in range(HEADS * HID // CHUNK // P):
-            nc.tensor.transpose(
-                rows_bank[:, block, :], bias[:, block * P : (block + 1) * P], ident_f32[:]
-            )
-        bias_rows = const.tile([P, 2 * STEP_PASSES, P], BF16)
-        nc.vector.tensor_copy(out=bias_rows[:], in_=rows_bank[:])
-
-        mask_bank = psum.tile([P, NTOK], F32, tag="hid_bank", bufs=4)
-        nc.tensor.matmul(mask_bank[:], lhsT=ones[:], rhs=mask_row[:], start=True, stop=True)
-        log_mask = const.tile([P, NTOK], F32)
-        nc.scalar.activation(out=log_mask[:], in_=mask_bank[:], func=ACT.Ln)
-        exp_first = const.tile([P, 1], F32)
-        nc.scalar.activation(out=exp_first[:], in_=log_mask[:, 0:1], func=ACT.Exp)
 
         pooled = const.tile([P, P], F32)
         nc.vector.memset(pooled[:], 0.0)
@@ -163,10 +142,16 @@ def tile_multiheadgeneralizedpooling_pa_k_kernel(
             w2_grouped = work.tile([P, STEP_PASSES * FEAT * PACK], BF16, align_bytes=64)
             w2_pairs = w2_grouped[:].bitcast(F32).rearrange("p (g d u) -> p g d u", d=FEAT, u=2)
             w2_planes = w2_bank[:].rearrange("p (g u) d -> p g d u", u=2)
-            nc.scalar.copy(out=w2_pairs, in_=w2_planes)
+            if step == 0:
+                nc.vector.tensor_copy(out=w2_pairs, in_=w2_planes)
+            else:
+                nc.scalar.copy(out=w2_pairs, in_=w2_planes)
             w2_grouped_tiles[step] = w2_grouped
             w1T = work.tile([P, STEP_CHUNKS, CHUNK], BF16)
-            nc.scalar.copy(out=w1T[:], in_=w1_bank[:])
+            if step == 0:
+                nc.vector.tensor_copy(out=w1T[:], in_=w1_bank[:])
+            else:
+                nc.scalar.copy(out=w1T[:], in_=w1_bank[:])
             w1T_tiles[step] = w1T
 
         def quantise_w2(step):
@@ -178,9 +163,9 @@ def tile_multiheadgeneralizedpooling_pa_k_kernel(
             w2_mx[step] = (w2_codes, w2_scales)
 
         def second_sentence(step):
-            if step % 2 == 1:
-                return "vector"
-            return "planes" if step % 8 == 6 else "bias matmul"
+            if step % 8 in (3, 6):
+                return "planes"
+            return "vector" if step % 2 == 1 else "bias matmul"
 
         def direct_tokens(step):
             return NTOK if second_sentence(step) == "vector" else TOKENS
@@ -355,6 +340,28 @@ def tile_multiheadgeneralizedpooling_pa_k_kernel(
                 op=ALU.mult,
             )
 
+        transpose_weights(0)
+        transpose_h(h_raw, SENTENCES, 0)
+        empty_weight_banks(0)
+
+        b_bank = psum.tile([P, 2 * STEP_PASSES, P], F32, tag="hid_bank", bufs=4)
+        b_words = b_raw[:].bitcast(F32)
+        for u in range(2):
+            nc.tensor.transpose(b_bank[:, u, :], b_words[:, u::2], ident_f32[:])
+        bias = const.tile([P, HEADS * HID // CHUNK], F32)
+        nc.vector.tensor_copy(
+            out=bias[:].rearrange("p (r u e) -> p r u e", u=2, e=2),
+            in_=b_bank[:].bitcast(BF16)[:, 0:2, :].rearrange("p u (r e) -> p r u e", e=2),
+        )
+
+        rows_bank = psum.tile([P, 2 * STEP_PASSES, P], F32, tag="hid_bank", bufs=4)
+        for block in range(HEADS * HID // CHUNK // P):
+            nc.tensor.transpose(
+                rows_bank[:, block, :], bias[:, block * P : (block + 1) * P], ident_f32[:]
+            )
+        bias_rows = const.tile([P, 2 * STEP_PASSES, P], BF16)
+        nc.vector.tensor_copy(out=bias_rows[:], in_=rows_bank[:])
+
         def is_step(step):
             return 0 <= step < STEPS
 
@@ -367,11 +374,10 @@ def tile_multiheadgeneralizedpooling_pa_k_kernel(
                 nc.gpsimd.tensor_scalar(
                     out=hT_f32[:], in0=hT_bf[:], scalar1=1.0, scalar2=0.0, op0=ALU.mult, op1=ALU.add
                 )
-            if is_step(r + 1):
-                if is_step(r + 1 + LOADS_AHEAD):
-                    raw_tiles[r + 1 + LOADS_AHEAD] = load_weights(r + 1 + LOADS_AHEAD)
+            if is_step(r + 1 + LOADS_AHEAD):
+                raw_tiles[r + 1 + LOADS_AHEAD] = load_weights(r + 1 + LOADS_AHEAD)
+            if r >= 0 and is_step(r + 1):
                 transpose_weights(r + 1)
-            if is_step(r + 1):
                 empty_weight_banks(r + 1)
             if is_step(r):
                 open_hidden(r)

@@ -30,6 +30,9 @@ STEP_CHUNKS = STEP_PASSES * PACK
 STEPS_PER_HEAD = HID // STEP_HID
 STEPS = HEADS * STEPS_PER_HEAD
 
+PAIR_PASSES = 2 * STEP_PASSES
+LAST_PAIR = STEPS // 2 - 1
+
 LOADS_AHEAD = 6
 
 REST_ROUND = 3
@@ -86,13 +89,6 @@ def tile_multiheadgeneralizedpooling_pa_k_kernel(
         ones = const.tile([P, P], BF16)
         nc.vector.memset(ones[:], 1.0)
 
-        mask_bank = psum.tile([P, NTOK], F32, tag="hid_bank", bufs=4)
-        nc.tensor.matmul(mask_bank[:], lhsT=ones[:], rhs=mask_row[:], start=True, stop=True)
-        log_mask = const.tile([P, NTOK], F32)
-        nc.scalar.activation(out=log_mask[:], in_=mask_bank[:], func=ACT.Ln)
-        exp_first = const.tile([P, 1], F32)
-        nc.scalar.activation(out=exp_first[:], in_=log_mask[:, 0:1], func=ACT.Exp)
-
         hT_bf = const.tile([P, HEADS * NTOK], BF16)
         hT_f32 = const.tile([P, HEADS * NTOK], F32)
 
@@ -139,39 +135,53 @@ def tile_multiheadgeneralizedpooling_pa_k_kernel(
 
         def empty_weight_banks(step):
             w1_bank, w2_bank = weight_banks[step]
-            w2_grouped = work.tile([P, STEP_PASSES * FEAT * PACK], BF16, align_bytes=64)
-            w2_pairs = w2_grouped[:].bitcast(F32).rearrange("p (g d u) -> p g d u", d=FEAT, u=2)
-            w2_planes = w2_bank[:].rearrange("p (g u) d -> p g d u", u=2)
-            if step == 0:
-                nc.vector.tensor_copy(out=w2_pairs, in_=w2_planes)
-            else:
-                nc.scalar.copy(out=w2_pairs, in_=w2_planes)
-            w2_grouped_tiles[step] = w2_grouped
             w1T = work.tile([P, STEP_CHUNKS, CHUNK], BF16)
             if step == 0:
                 nc.vector.tensor_copy(out=w1T[:], in_=w1_bank[:])
             else:
                 nc.scalar.copy(out=w1T[:], in_=w1_bank[:])
             w1T_tiles[step] = w1T
-
-        def quantise_w2(step):
-            w2_codes = codes.tile([P, STEP_PASSES * FEAT], U32, align_bytes=64)
-            w2_scales = codes.tile([P, STEP_PASSES * FEAT], U8, align_bytes=64)
-            nc.vector.quantize_mx(
-                out=w2_codes[:].bitcast(FP8X4), scales=w2_scales[:], in_=w2_grouped_tiles[step][:]
+            pair, half = divmod(step, 2)
+            if half == 0:
+                w2_grouped = work.tile([P, PAIR_PASSES * FEAT * PACK], BF16, align_bytes=64)
+                w2_grouped_tiles[pair] = w2_grouped
+            words = w2_grouped_tiles[pair][:].bitcast(F32)
+            width = STEP_PASSES * FEAT * 2
+            w2_pairs = words[:, half * width : (half + 1) * width].rearrange(
+                "p (g d u) -> p g d u", d=FEAT, u=2
             )
-            w2_mx[step] = (w2_codes, w2_scales)
+            w2_planes = w2_bank[:].rearrange("p (g u) d -> p g d u", u=2)
+            if step == 0:
+                nc.vector.tensor_copy(out=w2_pairs, in_=w2_planes)
+            else:
+                nc.scalar.copy(out=w2_pairs, in_=w2_planes)
 
-        def second_sentence(step):
-            if step % 8 in (3, 6):
-                return "planes"
-            return "vector" if step % 2 == 1 else "bias matmul"
+        def quantise_w2(pair):
+            w2_codes = codes.tile([P, PAIR_PASSES * FEAT], U32, align_bytes=64)
+            w2_scales = codes.tile([P, PAIR_PASSES * FEAT], U8, align_bytes=64)
+            nc.vector.quantize_mx(
+                out=w2_codes[:].bitcast(FP8X4), scales=w2_scales[:], in_=w2_grouped_tiles[pair][:]
+            )
+            w2_mx[pair] = (w2_codes, w2_scales)
 
-        def direct_tokens(step):
-            return NTOK if second_sentence(step) == "vector" else TOKENS
+        def other_sentence(step):
+            pair, half = divmod(step, 2)
+            if half == 0:
+                return "vector" if pair % 4 == 3 else "bias matmul"
+            return "planes" if pair % 2 == 0 else "vector"
 
-        def plane_columns(step):
-            return TOKENS if second_sentence(step) == "planes" else NTOK
+        def first_column(half, g):
+            return (2 * g + half) * NTOK
+
+        def direct_columns(pair):
+            first = 0 if other_sentence(2 * pair) == "vector" else TOKENS
+            last = 2 * NTOK if other_sentence(2 * pair + 1) == "vector" else 2 * NTOK - TOKENS
+            return first, last
+
+        PLANES_FROM = 2 * NTOK - TOKENS
+
+        def plane_columns(pair):
+            return PLANES_FROM if other_sentence(2 * pair + 1) == "planes" else 2 * NTOK
 
         def first_matmul(step, out_ap, chunk, tokens, alone=True, last=True):
             head = step // STEPS_PER_HEAD
@@ -183,29 +193,32 @@ def tile_multiheadgeneralizedpooling_pa_k_kernel(
                 stop=last,
             )
 
-        def open_hidden(step):
-            planes = work.tile([P, PACK, STEP_PASSES * NTOK], BF16)
-            plane_tiles[step] = planes
-            hid_grouped = work.tile([P, STEP_PASSES * NTOK * PACK], BF16, align_bytes=64)
-            hid_grouped_tiles[step] = hid_grouped
+        def open_hidden(pair):
+            planes = work.tile([P, PACK, PAIR_PASSES * NTOK - PLANES_FROM], BF16)
+            plane_tiles[pair] = planes
+            hid_grouped = work.tile([P, PAIR_PASSES * NTOK * PACK], BF16, align_bytes=64)
+            hid_grouped_tiles[pair] = hid_grouped
 
-        def hidden_direct(step):
+        def words_of(step, b):
+            pair, half = divmod(step, 2)
+            first = (first_column(half, 0) + b * TOKENS) * PACK
+            return hid_grouped_tiles[pair][:, first : first + TOKENS * PACK].rearrange(
+                "p (s t) -> p s t", t=PACK
+            )
+
+        def hidden_direct(step, b):
+            bank = psum.tile([P, PACK, TOKENS], F32, tag="hid_bank", bufs=4)
+            for t in range(PACK):
+                first_matmul(step, bank[:, t, :], t, slice(b * TOKENS, (b + 1) * TOKENS))
             column = step * STEP_CHUNKS
-            for b in range(direct_tokens(step) // TOKENS):
-                bank = psum.tile([P, PACK, TOKENS], F32, tag="hid_bank", bufs=4)
-                for t in range(PACK):
-                    first_matmul(step, bank[:, t, :], t, slice(b * TOKENS, (b + 1) * TOKENS))
-                words = hid_grouped_tiles[step][:, b * TOKENS * PACK : (b + 1) * TOKENS * PACK]
-                nc.vector.tensor_tensor(
-                    out=words.rearrange("p (s t) -> p s t", t=PACK),
-                    in0=bank[:].rearrange("p t s -> p s t"),
-                    in1=bias[:, column : column + PACK].unsqueeze(1).to_broadcast([P, TOKENS, PACK]),
-                    op=ALU.add,
-                )
+            nc.vector.tensor_tensor(
+                out=words_of(step, b),
+                in0=bank[:].rearrange("p t s -> p s t"),
+                in1=bias[:, column : column + PACK].unsqueeze(1).to_broadcast([P, TOKENS, PACK]),
+                op=ALU.add,
+            )
 
-        def hidden_biased(step):
-            if second_sentence(step) != "bias matmul":
-                return
+        def hidden_biased(step, b):
             bank = psum.tile([P, PACK, TOKENS], F32, tag="hid_bank", bufs=4)
             block, row = divmod(step * STEP_CHUNKS, P)
             nc.tensor.matmul(
@@ -217,78 +230,94 @@ def tile_multiheadgeneralizedpooling_pa_k_kernel(
             )
             for t in range(PACK):
                 first_matmul(
-                    step, bank[:, t, :], t, slice(TOKENS, NTOK), alone=False, last=t == PACK - 1
+                    step,
+                    bank[:, t, :],
+                    t,
+                    slice(b * TOKENS, (b + 1) * TOKENS),
+                    alone=False,
+                    last=t == PACK - 1,
                 )
-            words = hid_grouped_tiles[step][:, TOKENS * PACK : NTOK * PACK]
             nc.scalar.activation(
-                out=words.rearrange("p (s t) -> p s t", t=PACK),
-                in_=bank[:].rearrange("p t s -> p s t"),
-                func=ACT.Relu,
+                out=words_of(step, b), in_=bank[:].rearrange("p t s -> p s t"), func=ACT.Relu
             )
 
-        def relu_direct(step):
-            words = hid_grouped_tiles[step][:, 0 : direct_tokens(step) * PACK]
-            nc.vector.tensor_scalar_max(out=words, in0=words, scalar1=0.0)
-
-        def hidden_planes(step, g):
-            planes = plane_tiles[step]
-            first = plane_columns(step) if g == 0 else 0
-            width = NTOK - first
-            per_bank = 2 * NTOK // width if width else 0
-            for c in range(PACK if width else 0):
-                if c % per_bank == 0:
+        def hidden_planes(step, g, tokens):
+            pair, half = divmod(step, 2)
+            first = first_column(half, g) - PLANES_FROM
+            width = tokens.stop - tokens.start
+            per_bank = 2 * NTOK // width
+            for t in range(PACK):
+                if t % per_bank == 0:
                     bank = psum.tile([P, per_bank, width], F32, tag="hid_bank", bufs=4)
-                    for half in range(per_bank):
-                        first_matmul(
-                            step, bank[:, half, :], g * PACK + c + half, slice(first, NTOK)
-                        )
-                column = step * STEP_CHUNKS + g * PACK + c
+                    for i in range(per_bank):
+                        first_matmul(step, bank[:, i, :], g * PACK + t + i, tokens)
+                column = step * STEP_CHUNKS + g * PACK + t
                 nc.scalar.activation(
-                    out=planes[:, c, g * NTOK + first : (g + 1) * NTOK],
-                    in_=bank[:, c % per_bank, :],
+                    out=plane_tiles[pair][:, t, first + tokens.start : first + tokens.stop],
+                    in_=bank[:, t % per_bank, :],
                     func=ACT.Relu,
                     bias=bias[:, column : column + 1],
                     scale=1.0,
                 )
 
-        def group_hidden(step):
-            first = plane_columns(step)
+        def hidden_pass_0(step):
+            other = step % 2
+            hidden_direct(step, 1 - other)
+            way = other_sentence(step)
+            if way == "vector":
+                hidden_direct(step, other)
+            elif way == "bias matmul":
+                hidden_biased(step, other)
+            else:
+                hidden_planes(step, 0, slice(other * TOKENS, (other + 1) * TOKENS))
+
+        def relu_direct(pair, first, last):
+            words = hid_grouped_tiles[pair][:, first * PACK : last * PACK]
+            nc.vector.tensor_scalar_max(out=words, in0=words, scalar1=0.0)
+
+        def group_hidden(pair, first, last):
             nc.vector.tensor_copy(
-                out=hid_grouped_tiles[step][:, first * PACK :].rearrange(
+                out=hid_grouped_tiles[pair][:, first * PACK : last * PACK].rearrange(
                     "p (c i t) -> p c t i", i=4, t=PACK
                 ),
-                in_=plane_tiles[step][:, :, first:].rearrange("p t (c i) -> p c t i", i=4),
+                in_=plane_tiles[pair][:, :, first - PLANES_FROM : last - PLANES_FROM].rearrange(
+                    "p t (c i) -> p c t i", i=4
+                ),
             )
 
-        def quantise_hidden(step):
-            hid_codes = codes.tile([P, STEP_PASSES * NTOK], U32, align_bytes=64)
-            hid_scales = codes.tile([P, STEP_PASSES * NTOK], U8, align_bytes=64)
+        def open_codes(pair):
+            hid_codes = codes.tile([P, PAIR_PASSES * NTOK], U32, align_bytes=64)
+            hid_scales = codes.tile([P, PAIR_PASSES * NTOK], U8, align_bytes=64)
+            hid_mx[pair] = (hid_codes, hid_scales)
+
+        def quantise_hidden(pair, first, last):
+            hid_codes, hid_scales = hid_mx[pair]
             nc.vector.quantize_mx(
-                out=hid_codes[:].bitcast(FP8X4),
-                scales=hid_scales[:],
-                in_=hid_grouped_tiles[step][:],
+                out=hid_codes[:, first:last].bitcast(FP8X4),
+                scales=hid_scales[:, first:last],
+                in_=hid_grouped_tiles[pair][:, first * PACK : last * PACK],
             )
-            hid_mx[step] = (hid_codes, hid_scales)
 
-        def second_layer(step):
-            head, part = divmod(step, STEPS_PER_HEAD)
+        def second_layer(pair):
+            head, part = divmod(pair, STEPS_PER_HEAD // 2)
             if part == 0:
                 scores = psum.tile([P, NTOK], F32, tag="scores", bufs=1)
                 score_banks[head] = scores
             scores = score_banks[head]
-            w2_codes, w2_scales = w2_mx[step]
-            hid_codes, hid_scales = hid_mx[step]
-            for g in range(STEP_PASSES):
-                feats = slice(g * FEAT, (g + 1) * FEAT)
-                toks = slice(g * NTOK, (g + 1) * NTOK)
+            w2_codes, w2_scales = w2_mx[pair]
+            hid_codes, hid_scales = hid_mx[pair]
+            for i in range(PAIR_PASSES):
+                half, g = divmod(i, STEP_PASSES)
+                feats = slice(i * FEAT, (i + 1) * FEAT)
+                toks = slice(first_column(half, g), first_column(half, g) + NTOK)
                 nc.tensor.matmul_mx(
                     out=scores[:],
                     lhsT=w2_codes[:, feats].bitcast(FP8X4),
                     lhsT_scale=w2_scales[:, feats],
                     rhs=hid_codes[:, toks].bitcast(FP8X4),
                     rhs_scale=hid_scales[:, toks],
-                    start=(part == 0 and g == 0),
-                    stop=(part == STEPS_PER_HEAD - 1 and g == STEP_PASSES - 1),
+                    start=(part == 0 and i == 0),
+                    stop=(part == STEPS_PER_HEAD // 2 - 1 and i == PAIR_PASSES - 1),
                 )
 
         def softmax_shift(head):
@@ -344,6 +373,13 @@ def tile_multiheadgeneralizedpooling_pa_k_kernel(
         transpose_h(h_raw, SENTENCES, 0)
         empty_weight_banks(0)
 
+        mask_bank = psum.tile([P, NTOK], F32, tag="hid_bank", bufs=4)
+        nc.tensor.matmul(mask_bank[:], lhsT=ones[:], rhs=mask_row[:], start=True, stop=True)
+        log_mask = const.tile([P, NTOK], F32)
+        nc.scalar.activation(out=log_mask[:], in_=mask_bank[:], func=ACT.Ln)
+        exp_first = const.tile([P, 1], F32)
+        nc.scalar.activation(out=exp_first[:], in_=log_mask[:, 0:1], func=ACT.Exp)
+
         b_bank = psum.tile([P, 2 * STEP_PASSES, P], F32, tag="hid_bank", bufs=4)
         b_words = b_raw[:].bitcast(F32)
         for u in range(2):
@@ -354,21 +390,28 @@ def tile_multiheadgeneralizedpooling_pa_k_kernel(
             in_=b_bank[:].bitcast(BF16)[:, 0:2, :].rearrange("p u (r e) -> p r u e", e=2),
         )
 
-        rows_bank = psum.tile([P, 2 * STEP_PASSES, P], F32, tag="hid_bank", bufs=4)
-        for block in range(HEADS * HID // CHUNK // P):
-            nc.tensor.transpose(
-                rows_bank[:, block, :], bias[:, block * P : (block + 1) * P], ident_f32[:]
-            )
         bias_rows = const.tile([P, 2 * STEP_PASSES, P], BF16)
-        nc.vector.tensor_copy(out=bias_rows[:], in_=rows_bank[:])
+
+        def transpose_bias_rows():
+            bank = psum.tile([P, 2 * STEP_PASSES, P], F32, tag="hid_bank", bufs=4)
+            for block in range(2 * STEP_PASSES):
+                nc.tensor.transpose(
+                    bank[:, block, :], bias[:, block * P : (block + 1) * P], ident_f32[:]
+                )
+            nc.vector.tensor_copy(out=bias_rows[:], in_=bank[:])
 
         def is_step(step):
             return 0 <= step < STEPS
 
-        def ends_a_head(step):
-            return is_step(step) and step % STEPS_PER_HEAD == STEPS_PER_HEAD - 1
+        def is_pair(pair):
+            return 0 <= pair < STEPS // 2
 
-        for r in range(-1, STEPS + 4):
+        def ends_a_head(pair):
+            return is_pair(pair) and (pair + 1) % (STEPS_PER_HEAD // 2) == 0
+
+        for r in range(-1, STEPS + 7):
+            pair, half = divmod(r, 2)
+            head_done = (pair - 2) // (STEPS_PER_HEAD // 2)
             if r == REST_ROUND:
                 transpose_h(h_rest_raw, (HEADS - 1) * SENTENCES, SENTENCES)
                 nc.gpsimd.tensor_scalar(
@@ -379,29 +422,43 @@ def tile_multiheadgeneralizedpooling_pa_k_kernel(
             if r >= 0 and is_step(r + 1):
                 transpose_weights(r + 1)
                 empty_weight_banks(r + 1)
+            if r == 0:
+                transpose_bias_rows()
             if is_step(r):
-                open_hidden(r)
-                hidden_direct(r)
-                hidden_biased(r)
-                hidden_planes(r, 0)
-            if is_step(r - 3):
-                second_layer(r - 3)
-            if ends_a_head(r - 3):
-                softmax_shift((r - 3) // STEPS_PER_HEAD)
+                if half == 0:
+                    open_hidden(pair)
+                hidden_pass_0(r)
+            if half == 1 and is_pair(pair - 2):
+                second_layer(pair - 2)
+                if ends_a_head(pair - 2):
+                    softmax_shift(head_done)
             if is_step(r):
-                hidden_planes(r, 1)
-            if ends_a_head(r - 3):
-                softmax_exp((r - 3) // STEPS_PER_HEAD)
-            if is_step(r - 1):
-                group_hidden(r - 1)
-            if is_step(r + 1):
-                quantise_w2(r + 1)
-            if is_step(r):
-                relu_direct(r)
-            if is_step(r - 1):
-                quantise_hidden(r - 1)
-            if ends_a_head(r - 4):
-                weighted_sum((r - 4) // STEPS_PER_HEAD)
+                hidden_planes(r, 1, slice(0, NTOK))
+            if half == 1 and ends_a_head(pair - 2):
+                softmax_exp(head_done)
+            if half == 0 and is_pair(pair - 1) and pair - 1 != LAST_PAIR:
+                group_hidden(pair - 1, plane_columns(pair - 1), PAIR_PASSES * NTOK)
+                relu_direct(pair - 1, *direct_columns(pair - 1))
+            if half == 1 and is_pair(pair):
+                quantise_w2(pair)
+            if half == 1 and is_pair(pair - 1) and pair - 1 != LAST_PAIR:
+                open_codes(pair - 1)
+                quantise_hidden(pair - 1, 0, PAIR_PASSES * NTOK)
+            if r in (STEPS - 1, STEPS):
+                if r == STEPS - 1:
+                    open_codes(LAST_PAIR)
+                first, last = direct_columns(LAST_PAIR)
+                pass_0, pass_1 = first_column(r - STEPS + 1, 0), first_column(r - STEPS + 1, 1)
+                relu_direct(LAST_PAIR, max(first, pass_0), min(last, pass_0 + NTOK))
+                if r == STEPS - 1:
+                    group_hidden(LAST_PAIR, pass_1, pass_1 + NTOK)
+                    quantise_hidden(LAST_PAIR, pass_0, pass_0 + NTOK)
+                else:
+                    quantise_hidden(LAST_PAIR, pass_0, pass_0 + NTOK)
+                    group_hidden(LAST_PAIR, pass_1, pass_1 + NTOK)
+                quantise_hidden(LAST_PAIR, pass_1, pass_1 + NTOK)
+            if half == 0 and ends_a_head(pair - 3):
+                weighted_sum((pair - 3) // (STEPS_PER_HEAD // 2))
 
         out_bank = psum.tile([P, 2 * STEP_PASSES, P], F32, tag="w2_bank", bufs=1)
         nc.tensor.transpose(out_bank[:, 0, :], pooled[:], ident_f32[:])

@@ -167,7 +167,7 @@ def tile_multiheadgeneralizedpooling_pa_k_kernel(
         def other_sentence(step):
             pair, half = divmod(step, 2)
             if half == 0:
-                return "vector" if pair % 4 == 3 else "bias matmul"
+                return "vector" if pair % 4 == 3 and pair != LAST_PAIR else "bias matmul"
             return "planes" if pair % 2 == 0 else "vector"
 
         def first_column(half, g):
@@ -218,13 +218,29 @@ def tile_multiheadgeneralizedpooling_pa_k_kernel(
                 op=ALU.add,
             )
 
+        spread = {}
+
+        def make_spread(step):
+            row = step * STEP_CHUNKS % P
+            if other_sentence(step) == "bias matmul" and row not in spread:
+                ones_of_row = const.tile([P, PACK, TOKENS], BF16, name="spread_%d" % row)
+                nc.gpsimd.tensor_scalar(
+                    out=ones_of_row[:],
+                    in0=ident_bf[:, row : row + PACK].unsqueeze(2).to_broadcast([P, PACK, TOKENS]),
+                    scalar1=1.0,
+                    scalar2=0.0,
+                    op0=ALU.mult,
+                    op1=ALU.add,
+                )
+                spread[row] = ones_of_row
+
         def hidden_biased(step, b):
             bank = psum.tile([P, PACK, TOKENS], F32, tag="hid_bank", bufs=4)
             block, row = divmod(step * STEP_CHUNKS, P)
             nc.tensor.matmul(
                 bank[:],
                 lhsT=bias_rows[:, block, :],
-                rhs=ident_bf[:, row : row + PACK].unsqueeze(2).to_broadcast([P, PACK, TOKENS]),
+                rhs=spread[row][:],
                 start=True,
                 stop=False,
             )
@@ -390,6 +406,8 @@ def tile_multiheadgeneralizedpooling_pa_k_kernel(
             in_=b_bank[:].bitcast(BF16)[:, 0:2, :].rearrange("p u (r e) -> p r u e", e=2),
         )
 
+        for step in range(STEPS):
+            make_spread(step)
         bias_rows = const.tile([P, 2 * STEP_PASSES, P], BF16)
 
         def transpose_bias_rows():

@@ -133,14 +133,17 @@ def tile_multiheadgeneralizedpooling_pa_k_kernel(
                 )
             weight_banks[step] = (w1_bank, w2_bank)
 
-        def empty_weight_banks(step):
-            w1_bank, w2_bank = weight_banks[step]
+        def empty_w1_bank(step):
+            w1_bank = weight_banks[step][0]
             w1T = work.tile([P, STEP_CHUNKS, CHUNK], BF16)
             if step == 0:
                 nc.vector.tensor_copy(out=w1T[:], in_=w1_bank[:])
             else:
                 nc.scalar.copy(out=w1T[:], in_=w1_bank[:])
             w1T_tiles[step] = w1T
+
+        def empty_w2_bank(step):
+            w2_bank = weight_banks[step][1]
             pair, half = divmod(step, 2)
             if half == 0:
                 w2_grouped = work.tile([P, PAIR_PASSES * FEAT * PACK], BF16, align_bytes=64)
@@ -167,8 +170,8 @@ def tile_multiheadgeneralizedpooling_pa_k_kernel(
         def other_sentence(step):
             pair, half = divmod(step, 2)
             if half == 0:
-                return "vector" if pair % 4 == 3 and pair != LAST_PAIR else "bias matmul"
-            return "planes" if pair % 2 == 0 else "vector"
+                return "vector" if pair % 4 == 0 else "bias matmul"
+            return "planes" if pair % 4 == 0 or LAST_PAIR - 3 <= pair < LAST_PAIR else "vector"
 
         def first_column(half, g):
             return (2 * g + half) * NTOK
@@ -386,8 +389,8 @@ def tile_multiheadgeneralizedpooling_pa_k_kernel(
             )
 
         transpose_weights(0)
+        empty_w1_bank(0)
         transpose_h(h_raw, SENTENCES, 0)
-        empty_weight_banks(0)
 
         mask_bank = psum.tile([P, NTOK], F32, tag="hid_bank", bufs=4)
         nc.tensor.matmul(mask_bank[:], lhsT=ones[:], rhs=mask_row[:], start=True, stop=True)
@@ -406,6 +409,7 @@ def tile_multiheadgeneralizedpooling_pa_k_kernel(
             in_=b_bank[:].bitcast(BF16)[:, 0:2, :].rearrange("p u (r e) -> p r u e", e=2),
         )
 
+        empty_w2_bank(0)
         for step in range(STEPS):
             make_spread(step)
         bias_rows = const.tile([P, 2 * STEP_PASSES, P], BF16)
@@ -437,12 +441,16 @@ def tile_multiheadgeneralizedpooling_pa_k_kernel(
                 )
             if is_step(r + 1 + LOADS_AHEAD):
                 raw_tiles[r + 1 + LOADS_AHEAD] = load_weights(r + 1 + LOADS_AHEAD)
+            if r == 0:
+                open_hidden(0)
+                hidden_pass_0(0)
+            if r == 1:
+                transpose_bias_rows()
             if r >= 0 and is_step(r + 1):
                 transpose_weights(r + 1)
-                empty_weight_banks(r + 1)
-            if r == 0:
-                transpose_bias_rows()
-            if is_step(r):
+                empty_w1_bank(r + 1)
+                empty_w2_bank(r + 1)
+            if r > 0 and is_step(r):
                 if half == 0:
                     open_hidden(pair)
                 hidden_pass_0(r)

@@ -33,6 +33,9 @@ STEPS = HEADS * STEPS_PER_HEAD
 PAIR_PASSES = 2 * STEP_PASSES
 LAST_PAIR = STEPS // 2 - 1
 
+GPSIMD_COLUMNS = 128
+HANDOVER = 4
+
 LOADS_AHEAD = 6
 
 REST_ROUND = 3
@@ -61,15 +64,16 @@ def tile_multiheadgeneralizedpooling_pa_k_kernel(
                 out=w1_raw[:],
                 in_=W1[head, units, :].rearrange("(g p t) d -> p g (t d)", p=P, t=PACK),
             )
+            if step == 0:
+                nc.sync.dma_start(
+                    out=mask_row[0:1, :], in_=attention_mask.rearrange("b s -> (b s)").unsqueeze(0)
+                )
             w2_raw = raw.tile([P, STEP_HID], BF16)
             nc.sync.dma_start(out=w2_raw[:], in_=W2[head, :, units])
             return w1_raw, w2_raw
 
         mask_row = const.tile([P, NTOK], BF16)
         nc.gpsimd.memset(mask_row[:], 0.0)
-        nc.scalar.dma_start(
-            out=mask_row[0:1, :], in_=attention_mask.rearrange("b s -> (b s)").unsqueeze(0)
-        )
         raw_tiles = {0: load_weights(0)}
         h_view = h_heads.rearrange("i b s d -> s (i b) d")
         h_raw = const.tile([P, SENTENCES, FEAT], BF16)
@@ -88,9 +92,10 @@ def tile_multiheadgeneralizedpooling_pa_k_kernel(
         make_identity(nc, ident_f32[:])
         ones = const.tile([P, P], BF16)
         nc.vector.memset(ones[:], 1.0)
+        ln_first = const.tile([P, 1], F32)
+        nc.scalar.activation(out=ln_first[:], in_=ones[:, 0:1], func=ACT.Ln)
 
         hT_bf = const.tile([P, HEADS * NTOK], BF16)
-        hT_f32 = const.tile([P, HEADS * NTOK], F32)
 
         def transpose_h(source, count, first):
             bank = psum.tile([P, STEP_CHUNKS, P], BF16, tag="w1_bank", bufs=2)
@@ -104,7 +109,8 @@ def tile_multiheadgeneralizedpooling_pa_k_kernel(
         pooled = const.tile([P, P], F32)
         nc.vector.memset(pooled[:], 0.0)
 
-        weight_banks = {}
+        w1_banks = {}
+        w2_banks = {}
         w1T_tiles = {}
         w2_grouped_tiles = {}
         w2_mx = {}
@@ -115,15 +121,18 @@ def tile_multiheadgeneralizedpooling_pa_k_kernel(
         softmax_tiles = {}
         exp_tiles = {}
 
-        def transpose_weights(step):
-            w1_raw, w2_raw = raw_tiles[step]
+        def transpose_w1(step):
+            w1_raw = raw_tiles[step][0]
             w1_bank = psum.tile([P, STEP_CHUNKS, P], BF16, tag="w1_bank", bufs=2)
             for c in range(STEP_CHUNKS):
                 g, t = divmod(c, PACK)
                 nc.tensor.transpose(
                     w1_bank[:, c, :], w1_raw[:, g, t * FEAT : (t + 1) * FEAT], ident_bf[:]
                 )
-            w2_words = w2_raw[:].bitcast(F32)
+            w1_banks[step] = w1_bank
+
+        def transpose_w2(step):
+            w2_words = raw_tiles[step][1][:].bitcast(F32)
             w2_bank = psum.tile([P, 2 * STEP_PASSES, P], F32, tag="w2_bank", bufs=1)
             for gu in range(2 * STEP_PASSES):
                 g, u = divmod(gu, 2)
@@ -131,10 +140,10 @@ def tile_multiheadgeneralizedpooling_pa_k_kernel(
                 nc.tensor.transpose(
                     w2_bank[:, gu, :], w2_words[:, first + u : first + 2 * P : 2], ident_f32[:]
                 )
-            weight_banks[step] = (w1_bank, w2_bank)
+            w2_banks[step] = w2_bank
 
         def empty_w1_bank(step):
-            w1_bank = weight_banks[step][0]
+            w1_bank = w1_banks[step]
             w1T = work.tile([P, STEP_CHUNKS, CHUNK], BF16)
             if step == 0:
                 nc.vector.tensor_copy(out=w1T[:], in_=w1_bank[:])
@@ -143,7 +152,7 @@ def tile_multiheadgeneralizedpooling_pa_k_kernel(
             w1T_tiles[step] = w1T
 
         def empty_w2_bank(step):
-            w2_bank = weight_banks[step][1]
+            w2_bank = w2_banks[step]
             pair, half = divmod(step, 2)
             if half == 0:
                 w2_grouped = work.tile([P, PAIR_PASSES * FEAT * PACK], BF16, align_bytes=64)
@@ -167,24 +176,23 @@ def tile_multiheadgeneralizedpooling_pa_k_kernel(
             )
             w2_mx[pair] = (w2_codes, w2_scales)
 
-        def other_sentence(step):
+        def way(step, g, b):
             pair, half = divmod(step, 2)
-            if half == 0:
-                return "vector" if pair % 4 == 0 else "bias matmul"
-            return "planes" if pair % 4 == 0 or LAST_PAIR - 3 <= pair < LAST_PAIR else "vector"
+            if g == 1 or step == STEPS - 1:
+                return "planes"
+            return "bias matmul" if half == 0 and b == 0 and pair % 4 != 0 else "vector"
 
         def first_column(half, g):
             return (2 * g + half) * NTOK
 
         def direct_columns(pair):
-            first = 0 if other_sentence(2 * pair) == "vector" else TOKENS
-            last = 2 * NTOK if other_sentence(2 * pair + 1) == "vector" else 2 * NTOK - TOKENS
-            return first, last
-
-        PLANES_FROM = 2 * NTOK - TOKENS
+            first = 0 if way(2 * pair, 0, 0) == "vector" else TOKENS
+            return first, first_column(0 if pair == LAST_PAIR else 1, 0) + NTOK
 
         def plane_columns(pair):
-            return PLANES_FROM if other_sentence(2 * pair + 1) == "planes" else 2 * NTOK
+            return direct_columns(pair)[1], PAIR_PASSES * NTOK
+
+        PLANES_FROM = NTOK
 
         def first_matmul(step, out_ap, chunk, tokens, alone=True, last=True):
             head = step // STEPS_PER_HEAD
@@ -225,7 +233,7 @@ def tile_multiheadgeneralizedpooling_pa_k_kernel(
 
         def make_spread(step):
             row = step * STEP_CHUNKS % P
-            if other_sentence(step) == "bias matmul" and row not in spread:
+            if way(step, 0, 0) == "bias matmul" and row not in spread:
                 ones_of_row = const.tile([P, PACK, TOKENS], BF16, name="spread_%d" % row)
                 nc.gpsimd.tensor_scalar(
                     out=ones_of_row[:],
@@ -260,35 +268,32 @@ def tile_multiheadgeneralizedpooling_pa_k_kernel(
                 out=words_of(step, b), in_=bank[:].rearrange("p t s -> p s t"), func=ACT.Relu
             )
 
-        def hidden_planes(step, g, tokens):
+        def hidden_planes(step, g):
             pair, half = divmod(step, 2)
             first = first_column(half, g) - PLANES_FROM
-            width = tokens.stop - tokens.start
-            per_bank = 2 * NTOK // width
             for t in range(PACK):
-                if t % per_bank == 0:
-                    bank = psum.tile([P, per_bank, width], F32, tag="hid_bank", bufs=4)
-                    for i in range(per_bank):
-                        first_matmul(step, bank[:, i, :], g * PACK + t + i, tokens)
+                if t % 2 == 0:
+                    bank = psum.tile([P, 2, NTOK], F32, tag="hid_bank", bufs=4)
+                    for i in range(2):
+                        first_matmul(step, bank[:, i, :], g * PACK + t + i, slice(0, NTOK))
                 column = step * STEP_CHUNKS + g * PACK + t
                 nc.scalar.activation(
-                    out=plane_tiles[pair][:, t, first + tokens.start : first + tokens.stop],
-                    in_=bank[:, t % per_bank, :],
+                    out=plane_tiles[pair][:, t, first : first + NTOK],
+                    in_=bank[:, t % 2, :],
                     func=ACT.Relu,
                     bias=bias[:, column : column + 1],
                     scale=1.0,
                 )
 
         def hidden_pass_0(step):
-            other = step % 2
-            hidden_direct(step, 1 - other)
-            way = other_sentence(step)
-            if way == "vector":
-                hidden_direct(step, other)
-            elif way == "bias matmul":
-                hidden_biased(step, other)
-            else:
-                hidden_planes(step, 0, slice(other * TOKENS, (other + 1) * TOKENS))
+            if way(step, 0, 0) == "planes":
+                hidden_planes(step, 0)
+                return
+            for b in (1, 0) if step % 2 == 0 else (0, 1):
+                if way(step, 0, b) == "vector":
+                    hidden_direct(step, b)
+                else:
+                    hidden_biased(step, b)
 
         def relu_direct(pair, first, last):
             words = hid_grouped_tiles[pair][:, first * PACK : last * PACK]
@@ -302,6 +307,20 @@ def tile_multiheadgeneralizedpooling_pa_k_kernel(
                 in_=plane_tiles[pair][:, :, first - PLANES_FROM : last - PLANES_FROM].rearrange(
                     "p t (c i) -> p c t i", i=4
                 ),
+            )
+
+        def group_on_gpsimd(pair, first, last):
+            nc.gpsimd.tensor_scalar(
+                out=hid_grouped_tiles[pair][:, first * PACK : last * PACK].rearrange(
+                    "p (s t) -> p s t", t=PACK
+                ),
+                in0=plane_tiles[pair][:, :, first - PLANES_FROM : last - PLANES_FROM].rearrange(
+                    "p t s -> p s t"
+                ),
+                scalar1=1.0,
+                scalar2=0.0,
+                op0=ALU.mult,
+                op1=ALU.add,
             )
 
         def open_codes(pair):
@@ -370,27 +389,24 @@ def tile_multiheadgeneralizedpooling_pa_k_kernel(
 
         def weighted_sum(head):
             e, e_sum = exp_tiles[head]
-            he = small.tile([P, SENTENCES, TOKENS], F32)
-            nc.vector.tensor_tensor(
-                out=he[:].rearrange("p b s -> p (b s)"),
-                in0=e[:].rearrange("p b s -> p (b s)"),
-                in1=hT_f32[:, head * NTOK : (head + 1) * NTOK],
-                op=ALU.mult,
-            )
-            he_sum = small.tile([P, SENTENCES], F32)
-            nc.vector.tensor_reduce(out=he_sum[:], in_=he[:], axis=AXIS.X, op=ALU.add)
             inv_sum = small.tile([P, SENTENCES], F32)
             nc.vector.reciprocal(out=inv_sum[:], in_=e_sum[:])
-            nc.vector.tensor_tensor(
-                out=pooled[:, 0 : SENTENCES * HEADS].rearrange("p (b i) -> p b i", i=HEADS)[:, :, head],
-                in0=he_sum[:],
-                in1=inv_sum[:],
-                op=ALU.mult,
-            )
+            for b in range(SENTENCES):
+                tokens = slice(head * NTOK + b * TOKENS, head * NTOK + (b + 1) * TOKENS)
+                column = b * HEADS + head
+                weighted = small.tile([P, TOKENS], F32)
+                nc.vector.scalar_tensor_tensor(
+                    out=weighted[:],
+                    in0=e[:, b, :],
+                    scalar=inv_sum[:, b : b + 1],
+                    in1=hT_bf[:, tokens],
+                    op0=ALU.mult,
+                    op1=ALU.mult,
+                    accum_out=pooled[:, column : column + 1],
+                )
 
-        transpose_weights(0)
+        transpose_w1(0)
         empty_w1_bank(0)
-        transpose_h(h_raw, SENTENCES, 0)
 
         mask_bank = psum.tile([P, NTOK], F32, tag="hid_bank", bufs=4)
         nc.tensor.matmul(mask_bank[:], lhsT=ones[:], rhs=mask_row[:], start=True, stop=True)
@@ -398,6 +414,9 @@ def tile_multiheadgeneralizedpooling_pa_k_kernel(
         nc.scalar.activation(out=log_mask[:], in_=mask_bank[:], func=ACT.Ln)
         exp_first = const.tile([P, 1], F32)
         nc.scalar.activation(out=exp_first[:], in_=log_mask[:, 0:1], func=ACT.Exp)
+
+        transpose_w2(0)
+        transpose_h(h_raw, SENTENCES, 0)
 
         b_bank = psum.tile([P, 2 * STEP_PASSES, P], F32, tag="hid_bank", bufs=4)
         b_words = b_raw[:].bitcast(F32)
@@ -436,21 +455,20 @@ def tile_multiheadgeneralizedpooling_pa_k_kernel(
             head_done = (pair - 2) // (STEPS_PER_HEAD // 2)
             if r == REST_ROUND:
                 transpose_h(h_rest_raw, (HEADS - 1) * SENTENCES, SENTENCES)
-                nc.gpsimd.tensor_scalar(
-                    out=hT_f32[:], in0=hT_bf[:], scalar1=1.0, scalar2=0.0, op0=ALU.mult, op1=ALU.add
-                )
             if is_step(r + 1 + LOADS_AHEAD):
                 raw_tiles[r + 1 + LOADS_AHEAD] = load_weights(r + 1 + LOADS_AHEAD)
-            if r == 0:
-                open_hidden(0)
-                hidden_pass_0(0)
+            if is_step(r) and r < 2:
+                if half == 0:
+                    open_hidden(pair)
+                hidden_pass_0(r)
             if r == 1:
                 transpose_bias_rows()
             if r >= 0 and is_step(r + 1):
-                transpose_weights(r + 1)
+                transpose_w1(r + 1)
+                transpose_w2(r + 1)
                 empty_w1_bank(r + 1)
                 empty_w2_bank(r + 1)
-            if r > 0 and is_step(r):
+            if is_step(r) and r >= 2:
                 if half == 0:
                     open_hidden(pair)
                 hidden_pass_0(r)
@@ -459,12 +477,19 @@ def tile_multiheadgeneralizedpooling_pa_k_kernel(
                 if ends_a_head(pair - 2):
                     softmax_shift(head_done)
             if is_step(r):
-                hidden_planes(r, 1, slice(0, NTOK))
+                hidden_planes(r, 1)
             if half == 1 and ends_a_head(pair - 2):
                 softmax_exp(head_done)
             if half == 0 and is_pair(pair - 1) and pair - 1 != LAST_PAIR:
-                group_hidden(pair - 1, plane_columns(pair - 1), PAIR_PASSES * NTOK)
+                first, last = plane_columns(pair - 1)
+                shared = pair != LAST_PAIR
+                if shared:
+                    group_hidden(pair - 1, first, last - GPSIMD_COLUMNS + HANDOVER)
+                else:
+                    group_hidden(pair - 1, first, last)
                 relu_direct(pair - 1, *direct_columns(pair - 1))
+                if shared:
+                    group_on_gpsimd(pair - 1, last - GPSIMD_COLUMNS, last)
             if half == 1 and is_pair(pair):
                 quantise_w2(pair)
             if half == 1 and is_pair(pair - 1) and pair - 1 != LAST_PAIR:
@@ -473,15 +498,13 @@ def tile_multiheadgeneralizedpooling_pa_k_kernel(
             if r in (STEPS - 1, STEPS):
                 if r == STEPS - 1:
                     open_codes(LAST_PAIR)
-                first, last = direct_columns(LAST_PAIR)
                 pass_0, pass_1 = first_column(r - STEPS + 1, 0), first_column(r - STEPS + 1, 1)
-                relu_direct(LAST_PAIR, max(first, pass_0), min(last, pass_0 + NTOK))
                 if r == STEPS - 1:
-                    group_hidden(LAST_PAIR, pass_1, pass_1 + NTOK)
-                    quantise_hidden(LAST_PAIR, pass_0, pass_0 + NTOK)
+                    relu_direct(LAST_PAIR, *direct_columns(LAST_PAIR))
                 else:
-                    quantise_hidden(LAST_PAIR, pass_0, pass_0 + NTOK)
-                    group_hidden(LAST_PAIR, pass_1, pass_1 + NTOK)
+                    group_hidden(LAST_PAIR, pass_0, pass_0 + NTOK)
+                group_hidden(LAST_PAIR, pass_1, pass_1 + NTOK)
+                quantise_hidden(LAST_PAIR, pass_0, pass_0 + NTOK)
                 quantise_hidden(LAST_PAIR, pass_1, pass_1 + NTOK)
             if half == 0 and ends_a_head(pair - 3):
                 weighted_sum((pair - 3) // (STEPS_PER_HEAD // 2))

from contextlib import ExitStack

import concourse.mybir as mybir
from concourse.masks import make_identity

BF16 = mybir.dt.bfloat16
F32 = mybir.dt.float32
U32 = mybir.dt.uint32
U8 = mybir.dt.uint8
FP8X4 = mybir.dt.float8_e4m3fn_x4
ACT = mybir.ActivationFunctionType
ALU = mybir.AluOpType
AXIS = mybir.AxisListType

P = 128
HEADS = 4
SENTENCES = 2
TOKENS = 128
FEAT = 128
HID = 16384
NTOK = SENTENCES * TOKENS

PACK = 4
K_PASS = P * PACK
CHUNK = P

STEP_PASSES = 2
STEP_HID = STEP_PASSES * K_PASS
STEP_CHUNKS = STEP_PASSES * PACK
STEPS_PER_HEAD = HID // STEP_HID
STEPS = HEADS * STEPS_PER_HEAD

PAIR_PASSES = 2 * STEP_PASSES
LAST_PAIR = STEPS // 2 - 1

GPSIMD_COLUMNS = 128
HANDOVER = 4

LOADS_AHEAD = 6

REST_ROUND = 3

FLOPS = 2 * (2 * HEADS * NTOK * FEAT * HID)


def tile_multiheadgeneralizedpooling_pa_k_kernel(
    tc, h_heads, attention_mask, W1, b1, W2, out
):
    nc = tc.nc
    with ExitStack() as ctx:
        const = ctx.enter_context(tc.tile_pool(name="const", bufs=1))
        raw = ctx.enter_context(tc.tile_pool(name="raw", bufs=LOADS_AHEAD + 2))
        work = ctx.enter_context(tc.tile_pool(name="work", bufs=3))
        codes = ctx.enter_context(tc.tile_pool(name="codes", bufs=6))
        small = ctx.enter_context(tc.tile_pool(name="small", bufs=2))
        psum = ctx.enter_context(tc.psum_pool(name="psum", bufs=1))
        ctx.enter_context(tc.manual_schedule())

        def load_weights(step):
            head, part = divmod(step, STEPS_PER_HEAD)
            units = slice(part * STEP_HID, (part + 1) * STEP_HID)
            w1_raw = raw.tile([P, STEP_PASSES, PACK * FEAT], BF16)
            nc.sync.dma_start(
                out=w1_raw[:],
                in_=W1[head, units, :].rearrange("(g p t) d -> p g (t d)", p=P, t=PACK),
            )
            if step == 0:
                nc.sync.dma_start(
                    out=mask_row[0:1, :], in_=attention_mask.rearrange("b s -> (b s)").unsqueeze(0)
                )
            w2_raw = raw.tile([P, STEP_HID], BF16)
            nc.sync.dma_start(out=w2_raw[:], in_=W2[head, :, units])
            return w1_raw, w2_raw

        mask_row = const.tile([P, NTOK], BF16)
        nc.gpsimd.memset(mask_row[:], 0.0)
        raw_tiles = {0: load_weights(0)}
        h_view = h_heads.rearrange("i b s d -> s (i b) d")
        h_raw = const.tile([P, SENTENCES, FEAT], BF16)
        nc.sync.dma_start(out=h_raw[:], in_=h_view[:, 0:SENTENCES, :])
        b_raw = const.tile([P, K_PASS], BF16)
        nc.sync.dma_start(out=b_raw[:], in_=b1.rearrange("i (r c) -> (i r) c", c=K_PASS))
        raw_tiles[1] = load_weights(1)
        h_rest_raw = const.tile([P, (HEADS - 1) * SENTENCES, FEAT], BF16)
        nc.sync.dma_start(out=h_rest_raw[:], in_=h_view[:, SENTENCES:, :])
        for step in range(2, LOADS_AHEAD):
            raw_tiles[step] = load_weights(step)

        ident_bf = const.tile([P, P], BF16)
        make_identity(nc, ident_bf[:])
        ident_f32 = const.tile([P, P], F32)
        make_identity(nc, ident_f32[:])
        ones = const.tile([P, P], BF16)
        nc.vector.memset(ones[:], 1.0)
        ln_first = const.tile([P, 1], F32)
        nc.scalar.activation(out=ln_first[:], in_=ones[:, 0:1], func=ACT.Ln)

        hT_bf = const.tile([P, HEADS * NTOK], BF16)

        def transpose_h(source, count, first):
            bank = psum.tile([P, STEP_CHUNKS, P], BF16, tag="w1_bank", bufs=2)
            for ib in range(count):
                nc.tensor.transpose(bank[:, ib, :], source[:, ib, :], ident_bf[:])
            nc.vector.tensor_copy(
                out=hT_bf[:, first * P : (first + count) * P],
                in_=bank[:, 0:count, :].rearrange("p c s -> p (c s)"),
            )

        pooled = const.tile([P, P], F32)
        nc.vector.memset(pooled[:], 0.0)

        w1_banks = {}
        w2_banks = {}
        w1T_tiles = {}
        w2_grouped_tiles = {}
        w2_mx = {}
        plane_tiles = {}
        hid_grouped_tiles = {}
        hid_mx = {}
        score_banks = {}
        softmax_tiles = {}
        exp_tiles = {}

        def transpose_w1(step):
            w1_raw = raw_tiles[step][0]
            w1_bank = psum.tile([P, STEP_CHUNKS, P], BF16, tag="w1_bank", bufs=2)
            for c in range(STEP_CHUNKS):
                g, t = divmod(c, PACK)
                nc.tensor.transpose(
                    w1_bank[:, c, :], w1_raw[:, g, t * FEAT : (t + 1) * FEAT], ident_bf[:]
                )
            w1_banks[step] = w1_bank

        def transpose_w2(step):
            w2_words = raw_tiles[step][1][:].bitcast(F32)
            w2_bank = psum.tile([P, 2 * STEP_PASSES, P], F32, tag="w2_bank", bufs=1)
            for gu in range(2 * STEP_PASSES):
                g, u = divmod(gu, 2)
                first = g * 2 * P
                nc.tensor.transpose(
                    w2_bank[:, gu, :], w2_words[:, first + u : first + 2 * P : 2], ident_f32[:]
                )
            w2_banks[step] = w2_bank

        def empty_w1_bank(step):
            w1_bank = w1_banks[step]
            w1T = work.tile([P, STEP_CHUNKS, CHUNK], BF16)
            if step == 0:
                nc.vector.tensor_copy(out=w1T[:], in_=w1_bank[:])
            else:
                nc.scalar.copy(out=w1T[:], in_=w1_bank[:])
            w1T_tiles[step] = w1T

        def empty_w2_bank(step):
            w2_bank = w2_banks[step]
            pair, half = divmod(step, 2)
            if half == 0:
                w2_grouped = work.tile([P, PAIR_PASSES * FEAT * PACK], BF16, align_bytes=64)
                w2_grouped_tiles[pair] = w2_grouped
            words = w2_grouped_tiles[pair][:].bitcast(F32)
            width = STEP_PASSES * FEAT * 2
            w2_pairs = words[:, half * width : (half + 1) * width].rearrange(
                "p (g d u) -> p g d u", d=FEAT, u=2
            )
            w2_planes = w2_bank[:].rearrange("p (g u) d -> p g d u", u=2)
            if step == 0:
                nc.vector.tensor_copy(out=w2_pairs, in_=w2_planes)
            else:
                nc.scalar.copy(out=w2_pairs, in_=w2_planes)

        def quantise_w2(pair):
            w2_codes = codes.tile([P, PAIR_PASSES * FEAT], U32, align_bytes=64)
            w2_scales = codes.tile([P, PAIR_PASSES * FEAT], U8, align_bytes=64)
            nc.vector.quantize_mx(
                out=w2_codes[:].bitcast(FP8X4), scales=w2_scales[:], in_=w2_grouped_tiles[pair][:]
            )
            w2_mx[pair] = (w2_codes, w2_scales)

        def way(step, g, b):
            pair, half = divmod(step, 2)
            if g == 1 or step == STEPS - 1:
                return "planes"
            return "bias matmul" if half == 0 and b == 0 and pair % 4 != 0 else "vector"

        def first_column(half, g):
            return (2 * g + half) * NTOK

        def direct_columns(pair):
            first = 0 if way(2 * pair, 0, 0) == "vector" else TOKENS
            return first, first_column(0 if pair == LAST_PAIR else 1, 0) + NTOK

        def plane_columns(pair):
            return direct_columns(pair)[1], PAIR_PASSES * NTOK

        PLANES_FROM = NTOK

        def first_matmul(step, out_ap, chunk, tokens, alone=True, last=True):
            head = step // STEPS_PER_HEAD
            nc.tensor.matmul(
                out_ap,
                lhsT=w1T_tiles[step][:, chunk, :],
                rhs=hT_bf[:, head * NTOK + tokens.start : head * NTOK + tokens.stop],
                start=alone,
                stop=last,
            )

        def open_hidden(pair):
            planes = work.tile([P, PACK, PAIR_PASSES * NTOK - PLANES_FROM], BF16)
            plane_tiles[pair] = planes
            hid_grouped = work.tile([P, PAIR_PASSES * NTOK * PACK], BF16, align_bytes=64)
            hid_grouped_tiles[pair] = hid_grouped

        def words_of(step, b):
            pair, half = divmod(step, 2)
            first = (first_column(half, 0) + b * TOKENS) * PACK
            return hid_grouped_tiles[pair][:, first : first + TOKENS * PACK].rearrange(
                "p (s t) -> p s t", t=PACK
            )

        def hidden_direct(step, b):
            bank = psum.tile([P, PACK, TOKENS], F32, tag="hid_bank", bufs=4)
            for t in range(PACK):
                first_matmul(step, bank[:, t, :], t, slice(b * TOKENS, (b + 1) * TOKENS))
            column = step * STEP_CHUNKS
            nc.vector.tensor_tensor(
                out=words_of(step, b),
                in0=bank[:].rearrange("p t s -> p s t"),
                in1=bias[:, column : column + PACK].unsqueeze(1).to_broadcast([P, TOKENS, PACK]),
                op=ALU.add,
            )

        spread = {}

        def make_spread(step):
            row = step * STEP_CHUNKS % P
            if way(step, 0, 0) == "bias matmul" and row not in spread:
                ones_of_row = const.tile([P, PACK, TOKENS], BF16, name="spread_%d" % row)
                nc.gpsimd.tensor_scalar(
                    out=ones_of_row[:],
                    in0=ident_bf[:, row : row + PACK].unsqueeze(2).to_broadcast([P, PACK, TOKENS]),
                    scalar1=1.0,
                    scalar2=0.0,
                    op0=ALU.mult,
                    op1=ALU.add,
                )
                spread[row] = ones_of_row

        def hidden_biased(step, b):
            bank = psum.tile([P, PACK, TOKENS], F32, tag="hid_bank", bufs=4)
            block, row = divmod(step * STEP_CHUNKS, P)
            nc.tensor.matmul(
                bank[:],
                lhsT=bias_rows[:, block, :],
                rhs=spread[row][:],
                start=True,
                stop=False,
            )
            for t in range(PACK):
                first_matmul(
                    step,
                    bank[:, t, :],
                    t,
                    slice(b * TOKENS, (b + 1) * TOKENS),
                    alone=False,
                    last=t == PACK - 1,
                )
            nc.scalar.activation(
                out=words_of(step, b), in_=bank[:].rearrange("p t s -> p s t"), func=ACT.Relu
            )

        def hidden_planes(step, g):
            pair, half = divmod(step, 2)
            first = first_column(half, g) - PLANES_FROM
            for t in range(PACK):
                if t % 2 == 0:
                    bank = psum.tile([P, 2, NTOK], F32, tag="hid_bank", bufs=4)
                    for i in range(2):
                        first_matmul(step, bank[:, i, :], g * PACK + t + i, slice(0, NTOK))
                column = step * STEP_CHUNKS + g * PACK + t
                nc.scalar.activation(
                    out=plane_tiles[pair][:, t, first : first + NTOK],
                    in_=bank[:, t % 2, :],
                    func=ACT.Relu,
                    bias=bias[:, column : column + 1],
                    scale=1.0,
                )

        def hidden_pass_0(step):
            if way(step, 0, 0) == "planes":
                hidden_planes(step, 0)
                return
            for b in (1, 0) if step % 2 == 0 else (0, 1):
                if way(step, 0, b) == "vector":
                    hidden_direct(step, b)
                else:
                    hidden_biased(step, b)

        def relu_direct(pair, first, last):
            words = hid_grouped_tiles[pair][:, first * PACK : last * PACK]
            nc.vector.tensor_scalar_max(out=words, in0=words, scalar1=0.0)

        def group_hidden(pair, first, last):
            nc.vector.tensor_copy(
                out=hid_grouped_tiles[pair][:, first * PACK : last * PACK].rearrange(
                    "p (c i t) -> p c t i", i=4, t=PACK
                ),
                in_=plane_tiles[pair][:, :, first - PLANES_FROM : last - PLANES_FROM].rearrange(
                    "p t (c i) -> p c t i", i=4
                ),
            )

        def group_on_gpsimd(pair, first, last):
            nc.gpsimd.tensor_scalar(
                out=hid_grouped_tiles[pair][:, first * PACK : last * PACK].rearrange(
                    "p (s t) -> p s t", t=PACK
                ),
                in0=plane_tiles[pair][:, :, first - PLANES_FROM : last - PLANES_FROM].rearrange(
                    "p t s -> p s t"
                ),
                scalar1=1.0,
                scalar2=0.0,
                op0=ALU.mult,
                op1=ALU.add,
            )

        def open_codes(pair):
            hid_codes = codes.tile([P, PAIR_PASSES * NTOK], U32, align_bytes=64)
            hid_scales = codes.tile([P, PAIR_PASSES * NTOK], U8, align_bytes=64)
            hid_mx[pair] = (hid_codes, hid_scales)

        def quantise_hidden(pair, first, last):
            hid_codes, hid_scales = hid_mx[pair]
            nc.vector.quantize_mx(
                out=hid_codes[:, first:last].bitcast(FP8X4),
                scales=hid_scales[:, first:last],
                in_=hid_grouped_tiles[pair][:, first * PACK : last * PACK],
            )

        def second_layer(pair):
            head, part = divmod(pair, STEPS_PER_HEAD // 2)
            if part == 0:
                scores = psum.tile([P, NTOK], F32, tag="scores", bufs=1)
                score_banks[head] = scores
            scores = score_banks[head]
            w2_codes, w2_scales = w2_mx[pair]
            hid_codes, hid_scales = hid_mx[pair]
            for i in range(PAIR_PASSES):
                half, g = divmod(i, STEP_PASSES)
                feats = slice(i * FEAT, (i + 1) * FEAT)
                toks = slice(first_column(half, g), first_column(half, g) + NTOK)
                nc.tensor.matmul_mx(
                    out=scores[:],
                    lhsT=w2_codes[:, feats].bitcast(FP8X4),
                    lhsT_scale=w2_scales[:, feats],
                    rhs=hid_codes[:, toks].bitcast(FP8X4),
                    rhs_scale=hid_scales[:, toks],
                    start=(part == 0 and i == 0),
                    stop=(part == STEPS_PER_HEAD // 2 - 1 and i == PAIR_PASSES - 1),
                )

        def softmax_shift(head):
            neg_a = small.tile([P, SENTENCES, TOKENS], F32)
            nc.vector.scalar_tensor_tensor(
                out=neg_a[:].rearrange("p b s -> p (b s)"),
                in0=score_banks[head][:],
                scalar=-1.0,
                in1=log_mask[:],
                op0=ALU.mult,
                op1=ALU.subtract,
            )
            neg_max = small.tile([P, SENTENCES], F32)
            nc.vector.tensor_reduce(out=neg_max[:], in_=neg_a[:], axis=AXIS.X, op=ALU.min)
            softmax_tiles[head] = (neg_a, neg_max)

        def softmax_exp(head):
            neg_a, neg_max = softmax_tiles[head]
            e = small.tile([P, SENTENCES, TOKENS], F32)
            e_sum = small.tile([P, SENTENCES], F32)
            for b in range(SENTENCES):
                nc.scalar.activation(
                    out=e[:, b, :],
                    in_=neg_a[:, b, :],
                    func=ACT.Exp,
                    bias=neg_max[:, b : b + 1],
                    scale=-1.0,
                    accum_out=e_sum[:, b : b + 1],
                )
            exp_tiles[head] = (e, e_sum)

        def weighted_sum(head):
            e, e_sum = exp_tiles[head]
            inv_sum = small.tile([P, SENTENCES], F32)
            nc.vector.reciprocal(out=inv_sum[:], in_=e_sum[:])
            for b in range(SENTENCES):
                tokens = slice(head * NTOK + b * TOKENS, head * NTOK + (b + 1) * TOKENS)
                column = b * HEADS + head
                weighted = small.tile([P, TOKENS], F32)
                nc.vector.scalar_tensor_tensor(
                    out=weighted[:],
                    in0=e[:, b, :],
                    scalar=inv_sum[:, b : b + 1],
                    in1=hT_bf[:, tokens],
                    op0=ALU.mult,
                    op1=ALU.mult,
                    accum_out=pooled[:, column : column + 1],
                )

        transpose_w1(0)
        empty_w1_bank(0)

        mask_bank = psum.tile([P, NTOK], F32, tag="hid_bank", bufs=4)
        nc.tensor.matmul(mask_bank[:], lhsT=ones[:], rhs=mask_row[:], start=True, stop=True)
        log_mask = const.tile([P, NTOK], F32)
        nc.scalar.activation(out=log_mask[:], in_=mask_bank[:], func=ACT.Ln)
        exp_first = const.tile([P, 1], F32)
        nc.scalar.activation(out=exp_first[:], in_=log_mask[:, 0:1], func=ACT.Exp)

        transpose_w2(0)
        transpose_h(h_raw, SENTENCES, 0)

        b_bank = psum.tile([P, 2 * STEP_PASSES, P], F32, tag="hid_bank", bufs=4)
        b_words = b_raw[:].bitcast(F32)
        for u in range(2):
            nc.tensor.transpose(b_bank[:, u, :], b_words[:, u::2], ident_f32[:])
        bias = const.tile([P, HEADS * HID // CHUNK], F32)
        nc.vector.tensor_copy(
            out=bias[:].rearrange("p (r u e) -> p r u e", u=2, e=2),
            in_=b_bank[:].bitcast(BF16)[:, 0:2, :].rearrange("p u (r e) -> p r u e", e=2),
        )

        empty_w2_bank(0)
        for step in range(STEPS):
            make_spread(step)
        bias_rows = const.tile([P, 2 * STEP_PASSES, P], BF16)

        def transpose_bias_rows():
            bank = psum.tile([P, 2 * STEP_PASSES, P], F32, tag="hid_bank", bufs=4)
            for block in range(2 * STEP_PASSES):
                nc.tensor.transpose(
                    bank[:, block, :], bias[:, block * P : (block + 1) * P], ident_f32[:]
                )
            nc.vector.tensor_copy(out=bias_rows[:], in_=bank[:])

        def is_step(step):
            return 0 <= step < STEPS

        def is_pair(pair):
            return 0 <= pair < STEPS // 2

        def ends_a_head(pair):
            return is_pair(pair) and (pair + 1) % (STEPS_PER_HEAD // 2) == 0

        for r in range(-1, STEPS + 7):
            pair, half = divmod(r, 2)
            head_done = (pair - 2) // (STEPS_PER_HEAD // 2)
            if r == REST_ROUND:
                transpose_h(h_rest_raw, (HEADS - 1) * SENTENCES, SENTENCES)
            if is_step(r + 1 + LOADS_AHEAD):
                raw_tiles[r + 1 + LOADS_AHEAD] = load_weights(r + 1 + LOADS_AHEAD)
            if is_step(r) and r < 2:
                if half == 0:
                    open_hidden(pair)
                hidden_pass_0(r)
            if r == 1:
                transpose_bias_rows()
            if r >= 0 and is_step(r + 1):
                transpose_w1(r + 1)
                transpose_w2(r + 1)
                empty_w1_bank(r + 1)
                empty_w2_bank(r + 1)
            if is_step(r) and r >= 2:
                if half == 0:
                    open_hidden(pair)
                hidden_pass_0(r)
            if half == 1 and is_pair(pair - 2):
                second_layer(pair - 2)
                if ends_a_head(pair - 2):
                    softmax_shift(head_done)
            if is_step(r):
                hidden_planes(r, 1)
            if half == 1 and ends_a_head(pair - 2):
                softmax_exp(head_done)
            if half == 0 and is_pair(pair - 1) and pair - 1 != LAST_PAIR:
                first, last = plane_columns(pair - 1)
                shared = pair != LAST_PAIR
                if shared:
                    group_hidden(pair - 1, first, last - GPSIMD_COLUMNS + HANDOVER)
                else:
                    group_hidden(pair - 1, first, last)
                relu_direct(pair - 1, *direct_columns(pair - 1))
                if shared:
                    group_on_gpsimd(pair - 1, last - GPSIMD_COLUMNS, last)
            if half == 1 and is_pair(pair):
                quantise_w2(pair)
            if half == 1 and is_pair(pair - 1) and pair - 1 != LAST_PAIR:
                open_codes(pair - 1)
                quantise_hidden(pair - 1, 0, PAIR_PASSES * NTOK)
            if r in (STEPS - 1, STEPS):
                if r == STEPS - 1:
                    open_codes(LAST_PAIR)
                pass_0, pass_1 = first_column(r - STEPS + 1, 0), first_column(r - STEPS + 1, 1)
                if r == STEPS - 1:
                    relu_direct(LAST_PAIR, *direct_columns(LAST_PAIR))
                else:
                    group_hidden(LAST_PAIR, pass_0, pass_0 + NTOK)
                group_hidden(LAST_PAIR, pass_1, pass_1 + NTOK)
                quantise_hidden(LAST_PAIR, pass_0, pass_0 + NTOK)
                quantise_hidden(LAST_PAIR, pass_1, pass_1 + NTOK)
            if half == 0 and ends_a_head(pair - 3):
                weighted_sum((pair - 3) // (STEPS_PER_HEAD // 2))

        out_bank = psum.tile([P, 2 * STEP_PASSES, P], F32, tag="w2_bank", bufs=1)
        nc.tensor.transpose(out_bank[:, 0, :], pooled[:], ident_f32[:])
        out_rows = small.tile([P, FEAT], F32)
        nc.vector.tensor_copy(out=out_rows[:], in_=out_bank[:, 0, :])
        nc.sync.dma_start(
            out=out.rearrange("b (i d) -> (b i) d", d=FEAT), in_=out_rows[0 : SENTENCES * HEADS, :]
        )
